import numpy as np
import ml_dtypes


def mxq(x, axis, fmt="e4m3"):
    dtype, down = {"e4m3": (ml_dtypes.float8_e4m3fn, 7), "e5m2": (ml_dtypes.float8_e5m2, 14)}[fmt]
    v = np.moveaxis(np.asarray(x, np.float32).astype(ml_dtypes.bfloat16).astype(np.float64), axis, -1)
    blocks = v.reshape(v.shape[:-1] + (-1, 32))
    amax = np.abs(blocks).max(-1, keepdims=True)
    byte = np.maximum(np.where(amax > 0, np.frexp(amax)[1] - 1 + 127, 0) - down, 1)
    scale = np.exp2(byte - 127.0)
    codes = (blocks / scale).astype(np.float32).astype(dtype).astype(np.float64)
    return np.moveaxis((codes * scale).reshape(v.shape), -1, axis)


BF16 = ml_dtypes.bfloat16


def bf(x):
    return np.asarray(x, np.float32).astype(BF16)


def f64(x):
    return np.asarray(x).astype(np.float64)


B, C, H, W, N, K, R = 16, 512, 32, 32, 4, 32, 8

ENSEMBLE_MAX_MEAN = 0.5
EPS = 1e-12


def _l2norm(x, axis):
    return x / np.sqrt(np.sum(x * x, axis=axis, keepdims=True) + EPS)


def setup_inputs():
    g = np.random.standard_normal((R, C)) / np.sqrt(R)
    x = np.random.standard_normal((B, C, H, W))
    p = np.random.standard_normal((N, K, C))
    for r in range(R):
        x += np.random.standard_normal((B, 1, H, W)) * g[r][None, :, None, None]
        p += (np.random.standard_normal((N, 1, 1)) + np.random.standard_normal((N, K, 1))) * np.sqrt(0.5) * g[r]
    return {"image_feat": bf(x), "proto_emb": bf(p)}


def reference(image_feat, proto_emb):
    img = _l2norm(f64(image_feat), 1)
    pro = _l2norm(f64(proto_emb), -1)
    imgq = mxq(img, 1, "e4m3").reshape(B, C, H * W)
    proq = mxq(pro, 2, "e4m3").reshape(N * K, C)
    simmap = (proq @ imgq).reshape(B, N, K, H, W)
    sim_max = np.max(simmap, axis=2)
    sim_mean = np.mean(simmap, axis=2)
    sim = ENSEMBLE_MAX_MEAN * sim_max + (1.0 - ENSEMBLE_MAX_MEAN) * sim_mean
    soft_mask = 1.0 / (1.0 + np.exp(-sim))
    return soft_mask, sim

@@ -1,0 +1,264 @@
+from contextlib import ExitStack
+
+import concourse.mybir as mybir
+from concourse.masks import make_identity
+
+FLOPS = 2 * 16384 * 512 * 128
+
+BF16 = mybir.dt.bfloat16
+F32 = mybir.dt.float32
+U32 = mybir.dt.uint32
+U8 = mybir.dt.uint8
+FP8X4 = mybir.dt.float8_e4m3fn_x4
+ACT = mybir.ActivationFunctionType
+ALU = mybir.AluOpType
+AX = mybir.AxisListType
+
+P = 128
+NB = 16
+NG = 32
+MANUAL = False
+MV = 160
+
+
+def tile_freedamasker_t_kernel(tc, image_feat, proto_emb, out_0, out_1):
+    nc = tc.nc
+    with ExitStack() as ctx:
+        keep = ctx.enter_context(tc.tile_pool(name="keep", bufs=1))
+        small = ctx.enter_context(tc.tile_pool(name="small", bufs=8))
+        work = ctx.enter_context(tc.tile_pool(name="work", bufs=2))
+        grpool = ctx.enter_context(tc.tile_pool(name="grpool", bufs=1))
+        ps_xt = ctx.enter_context(tc.psum_pool(name="ps_xt", bufs=3))
+        ps_r = ctx.enter_context(tc.psum_pool(name="ps_r", bufs=3))
+        ps_o = ctx.enter_context(tc.psum_pool(name="ps_o", bufs=2))
+
+        pro = keep.tile([P, 512], BF16, name="pro")
+        nc.scalar.dma_start(out=pro[:], in_=proto_emb.rearrange("n k c -> (n k) c"))
+        xs = []
+        for b in range(NB):
+            xb = keep.tile([P, 4, 1024], BF16, name="x%d" % b)
+            src = image_feat[b].rearrange("(p t) h w -> p t (h w)", t=4)
+            if b == 0:
+                for lo, hi in ((0, 256), (256, 512), (512, 1024)):
+                    nc.sync.dma_start(out=xb[:, :, lo:hi], in_=src[:, :, lo:hi])
+            else:
+                nc.sync.dma_start(out=xb[:], in_=src)
+            xs.append(xb)
+
+        eps = keep.tile([P, 1], F32, name="eps")
+        nc.vector.memset(eps[:], 1e-12)
+        warm = keep.tile([P, 1], F32, name="warm")
+        nc.scalar.activation(out=warm[:], in_=eps[:], func=ACT.Sqrt)
+        ident_f = keep.tile([P, P], F32, name="ident_f")
+        make_identity(nc, ident_f[:])
+        ident_b = keep.tile([P, P], BF16, name="ident_b")
+        make_identity(nc, ident_b[:])
+
+        res_max = keep.tile([P, 512], F32, name="res_max")
+        res_sum = keep.tile([P, 512], F32, name="res_sum")
+        res_max_v = res_max[:].rearrange("p (b n a) -> p b n a", n=4, a=8)
+        res_sum_v = res_sum[:].rearrange("p (b n a) -> p b n a", n=4, a=8)
+        sim_t = keep.tile([P, 512], F32, name="sim_t")
+        sim_sb = keep.tile([P, 512], F32, name="sim_sb")
+        mask_sb = keep.tile([P, 512], F32, name="mask_sb")
+        dst0 = out_0.rearrange("b n (a r) w -> (b n a) (r w)", a=8).rearrange("(q p) f -> p q f", p=P)
+        dst1 = out_1.rearrange("b n (a r) w -> (b n a) (r w)", a=8).rearrange("(q p) f -> p q f", p=P)
+
+        pjunk = keep.tile([P, 512], BF16, name="pjunk")
+        pss = keep.tile([P, 1], F32, name="pss")
+        nc.scalar.activation(out=pjunk[:], in_=pro[:], func=ACT.Square, accum_out=pss[:])
+        pnrm = keep.tile([P, 1], F32, name="pnrm")
+        nc.scalar.activation(out=pnrm[:], in_=pss[:], func=ACT.Sqrt, bias=eps[:, 0:1])
+        prin = keep.tile([P, 1], F32, name="prin")
+        nc.vector.reciprocal(out=prin[:], in_=pnrm[:])
+        pn = keep.tile([P, 4, P], BF16, name="pn")
+        nc.vector.tensor_scalar(
+            out=pn[:], in0=pro[:].rearrange("m (p t) -> m t p", t=4),
+            scalar1=prin[:, 0:1], scalar2=None, op0=ALU.mult,
+        )
+        pt_ps = ps_o.tile([P, 4, P], BF16, name="o")
+        for t in range(4):
+            nc.tensor.transpose(pt_ps[:, t, :], pn[:, t, :], ident_b[:])
+        pgrp = keep.tile([P, P, 4], BF16, name="pgrp", align_bytes=64)
+        nc.vector.tensor_copy(out=pgrp[:], in_=pt_ps[:].rearrange("p t m -> p m t"))
+        pcodes = keep.tile([P, P], U32, name="pcodes", align_bytes=64)
+        pscl = keep.tile([P, P], U8, name="pscl", align_bytes=64)
+        nc.vector.quantize_mx(
+            out=pcodes[:].bitcast(FP8X4), scales=pscl[:],
+            in_=pgrp[:].rearrange("p m t -> p (m t)"),
+        )
+
+        xts = {}
+        sss = {}
+        nrms = {}
+        rins = {}
+        rbs = {}
+        rss = {}
+        grps = {}
+        cds = {}
+        outs = {}
+
+        def t1(g):
+            b, half = divmod(g, 2)
+            xw = xs[b][:].bitcast(F32)
+            banks = []
+            for k in range(2):
+                xt = ps_xt.tile([P, 512], F32, name="xt")
+                w0 = 256 * half + 128 * k
+                for t in range(4):
+                    nc.tensor.transpose(
+                        xt[:, 128 * t:128 * (t + 1)], xw[:, t, w0:w0 + 128], ident_f[:]
+                    )
+                banks.append(xt)
+            xts[g] = banks
+            sss[g] = small.tile([P, 4], F32, name="ss")
+
+        def sumsq(g, k):
+            v = xts[g][k][:].bitcast(BF16).rearrange("p (c e) -> p c e", e=2)
+            for e in range(2):
+                junk = work.tile([P, 512], BF16, name="junk")
+                nc.scalar.activation(
+                    out=junk[:], in_=v[:, :, e], func=ACT.Square,
+                    accum_out=sss[g][:, 2 * k + e:2 * k + e + 1],
+                )
+
+        def root(g):
+            nrm = small.tile([P, 4], F32, name="nrm")
+            nc.scalar.activation(out=nrm[:], in_=sss[g][:], func=ACT.Sqrt, bias=eps[:, 0:1])
+            nrms[g] = nrm
+
+        def recip(g):
+            rin = small.tile([P, 4], F32, name="rin")
+            nc.vector.reciprocal(out=rin[:], in_=nrms[g][:])
+            rins[g] = rin
+
+        def bcast_t(g):
+            rp = ps_r.tile([P, 2, 256], F32, name="rp")
+            for k in range(2):
+                for e in range(2):
+                    c = 2 * k + e
+                    nc.tensor.transpose(
+                        rp[:, e, 128 * k:128 * (k + 1)],
+                        rins[g][:, c:c + 1].to_broadcast([P, P]), ident_f[:],
+                    )
+            rbs[g] = rp
+
+        def rcopy(g):
+            if MV < 256:
+                rs = work.tile([P, 256 - MV, 2], F32, name="rs")
+                nc.scalar.copy(out=rs[:], in_=rbs[g][:, :, MV:256].rearrange("p e m -> p m e"))
+                rss[g] = rs
+
+        def scale(g):
+            b, half = divmod(g, 2)
+            grp = grpool.tile([P, 2048], BF16, name="grp", align_bytes=64)
+            w0 = 512 * half
+            if MV < 256:
+                nw = 2 * (256 - MV)
+                nc.gpsimd.tensor_tensor(
+                    out=grp[:, 8 * MV:2048].rearrange("p (w t) -> p w t", t=4),
+                    in0=xs[b][:, :, w0 + 2 * MV:w0 + 512].rearrange("p t w -> p w t"),
+                    in1=rss[g][:].rearrange("p m e -> p (m e)").unsqueeze(2).to_broadcast([P, nw, 4]),
+                    op=ALU.mult,
+                )
+            nc.vector.tensor_tensor(
+                out=grp[:, 0:8 * MV].rearrange("p (m e t) -> p m e t", e=2, t=4),
+                in0=xs[b][:, :, w0:w0 + 2 * MV].rearrange("p t (m e) -> p m e t", e=2),
+                in1=rbs[g][:, :, 0:MV].rearrange("p e m -> p m e").unsqueeze(3).to_broadcast([P, MV, 2, 4]),
+                op=ALU.mult,
+            )
+            grps[g] = grp
+
+        def quant(g):
+            codes = work.tile([P, 512], U32, name="codes", align_bytes=64)
+            scl = work.tile([P, 512], U8, name="scl", align_bytes=64)
+            nc.vector.quantize_mx(out=codes[:].bitcast(FP8X4), scales=scl[:], in_=grps[g][:])
+            cds[g] = (codes, scl)
+
+        def mx(g):
+            codes, scl = cds[g]
+            o = ps_o.tile([P, 512], F32, name="o")
+            for j in range(4):
+                cols = slice(128 * j, 128 * (j + 1))
+                nc.tensor.matmul_mx(
+                    out=o[:, cols],
+                    lhsT=codes[:, cols].bitcast(FP8X4), lhsT_scale=scl[:, cols],
+                    rhs=pcodes[:].bitcast(FP8X4), rhs_scale=pscl[:],
+                    start=True, stop=True,
+                )
+            outs[g] = o
+
+        def reduce(g):
+            b, half = divmod(g, 2)
+            ov = outs[g][:].rearrange("p (j n k) -> p j n k", n=4, k=32)
+            a0 = 4 * half
+            nc.vector.tensor_reduce(
+                out=res_max_v[:, b, :, a0:a0 + 4].rearrange("p n j -> p j n"),
+                in_=ov, axis=AX.X, op=ALU.max,
+            )
+            nc.vector.tensor_reduce(
+                out=res_sum_v[:, b, :, a0:a0 + 4].rearrange("p n j -> p j n"),
+                in_=ov, axis=AX.X, op=ALU.add,
+            )
+
+        def mix(q):
+            cols = slice(128 * q, 128 * (q + 1))
+            tmp = work.tile([P, P], F32, name="tmp")
+            nc.vector.tensor_scalar(
+                out=tmp[:], in0=res_sum[:, cols], scalar1=1.0 / 64.0, scalar2=None, op0=ALU.mult
+            )
+            nc.vector.scalar_tensor_tensor(
+                out=sim_t[:, cols], in0=res_max[:, cols], scalar=0.5, in1=tmp[:],
+                op0=ALU.mult, op1=ALU.add,
+            )
+            fin = ps_o.tile([P, P], F32, name="o")
+            nc.tensor.transpose(fin[:], sim_t[:, cols], ident_f[:])
+            return fin
+
+        def ok(g):
+            return 0 <= g < NG
+
+        def body():
+            for i in range(-5, NG):
+                if ok(i):
+                    quant(i)
+                if ok(i + 1):
+                    scale(i + 1)
+                if ok(i + 2):
+                    bcast_t(i + 2)
+                if ok(i + 4):
+                    sumsq(i + 4, 0)
+                if ok(i + 2):
+                    rcopy(i + 2)
+                if ok(i + 4):
+                    sumsq(i + 4, 1)
+                    root(i + 4)
+                if ok(i):
+                    mx(i)
+                if ok(i + 5):
+                    t1(i + 5)
+                if ok(i):
+                    reduce(i)
+                if ok(i + 3):
+                    recip(i + 3)
+                if ok(i) and i % 8 == 7 and i < NG - 1:
+                    q = i // 8
+                    fin = mix(q)
+                    nc.scalar.copy(out=sim_sb[:, 128 * q:128 * (q + 1)], in_=fin[:])
+                    nc.sync.dma_start(out=dst1[:, q, :], in_=sim_sb[:, 128 * q:128 * (q + 1)])
+
+        if MANUAL:
+            with tc.manual_schedule():
+                body()
+        else:
+            body()
+
+        nc.scalar.activation(out=mask_sb[:, 0:384], in_=sim_sb[:, 0:384], func=ACT.Sigmoid)
+        nc.sync.dma_start(
+            out=dst0[:, 0:3, :], in_=mask_sb[:, 0:384].rearrange("p (q f) -> p q f", q=3)
+        )
+        fin = mix(3)
+        nc.scalar.activation(out=mask_sb[:, 384:512], in_=fin[:], func=ACT.Sigmoid)
+        nc.vector.tensor_copy(out=sim_sb[:, 384:512], in_=fin[:])
+        nc.sync.dma_start(out=dst0[:, 3, :], in_=mask_sb[:, 384:512])
+        nc.scalar.dma_start(out=dst1[:, 3, :], in_=sim_sb[:, 384:512])

@@ -18,7 +18,7 @@ P = 128
 NB = 16
 NG = 32
 MANUAL = False
-MV = 160
+MV = 192
 
 
 def tile_freedamasker_t_kernel(tc, image_feat, proto_emb, out_0, out_1):
@@ -27,7 +27,7 @@ def tile_freedamasker_t_kernel(tc, image_feat, proto_emb, out_0, out_1):
         keep = ctx.enter_context(tc.tile_pool(name="keep", bufs=1))
         small = ctx.enter_context(tc.tile_pool(name="small", bufs=8))
         work = ctx.enter_context(tc.tile_pool(name="work", bufs=2))
-        grpool = ctx.enter_context(tc.tile_pool(name="grpool", bufs=1))
+        grpool = ctx.enter_context(tc.tile_pool(name="grpool", bufs=2))
         ps_xt = ctx.enter_context(tc.psum_pool(name="ps_xt", bufs=3))
         ps_r = ctx.enter_context(tc.psum_pool(name="ps_r", bufs=3))
         ps_o = ctx.enter_context(tc.psum_pool(name="ps_o", bufs=2))
@@ -149,9 +149,10 @@ def tile_freedamasker_t_kernel(tc, image_feat, proto_emb, out_0, out_1):
                 nc.scalar.copy(out=rs[:], in_=rbs[g][:, :, MV:256].rearrange("p e m -> p m e"))
                 rss[g] = rs
 
-        def scale(g):
+        def scale_g(g):
             b, half = divmod(g, 2)
             grp = grpool.tile([P, 2048], BF16, name="grp", align_bytes=64)
+            grps[g] = grp
             w0 = 512 * half
             if MV < 256:
                 nw = 2 * (256 - MV)
@@ -161,13 +162,17 @@ def tile_freedamasker_t_kernel(tc, image_feat, proto_emb, out_0, out_1):
                     in1=rss[g][:].rearrange("p m e -> p (m e)").unsqueeze(2).to_broadcast([P, nw, 4]),
                     op=ALU.mult,
                 )
+
+        def scale_v(g):
+            b, half = divmod(g, 2)
+            grp = grps[g]
+            w0 = 512 * half
             nc.vector.tensor_tensor(
                 out=grp[:, 0:8 * MV].rearrange("p (m e t) -> p m e t", e=2, t=4),
                 in0=xs[b][:, :, w0:w0 + 2 * MV].rearrange("p t (m e) -> p m e t", e=2),
                 in1=rbs[g][:, :, 0:MV].rearrange("p e m -> p m e").unsqueeze(3).to_broadcast([P, MV, 2, 4]),
                 op=ALU.mult,
             )
-            grps[g] = grp
 
         def quant(g):
             codes = work.tile([P, 512], U32, name="codes", align_bytes=64)
@@ -219,28 +224,30 @@ def tile_freedamasker_t_kernel(tc, image_feat, proto_emb, out_0, out_1):
             return 0 <= g < NG
 
         def body():
-            for i in range(-5, NG):
+            for i in range(-6, NG):
                 if ok(i):
                     quant(i)
+                if ok(i + 2):
+                    scale_g(i + 2)
                 if ok(i + 1):
-                    scale(i + 1)
-                if ok(i + 2):
-                    bcast_t(i + 2)
-                if ok(i + 4):
-                    sumsq(i + 4, 0)
-                if ok(i + 2):
-                    rcopy(i + 2)
-                if ok(i + 4):
-                    sumsq(i + 4, 1)
-                    root(i + 4)
+                    scale_v(i + 1)
+                if ok(i + 3):
+                    bcast_t(i + 3)
+                if ok(i + 5):
+                    sumsq(i + 5, 0)
+                if ok(i + 3):
+                    rcopy(i + 3)
+                if ok(i + 5):
+                    sumsq(i + 5, 1)
+                    root(i + 5)
                 if ok(i):
                     mx(i)
-                if ok(i + 5):
-                    t1(i + 5)
+                if ok(i + 6):
+                    t1(i + 6)
                 if ok(i):
                     reduce(i)
-                if ok(i + 3):
-                    recip(i + 3)
+                if ok(i + 4):
+                    recip(i + 4)
                 if ok(i) and i % 8 == 7 and i < NG - 1:
                     q = i // 8
                     fin = mix(q)

@@ -17,7 +17,7 @@ AX = mybir.AxisListType
 P = 128
 NB = 16
 NG = 32
-MANUAL = False
+MANUAL = True
 MV = 192
 
 

@@ -16,9 +16,9 @@ AX = mybir.AxisListType
 
 P = 128
 NB = 16
-NG = 32
-MANUAL = True
-MV = 192
+MANUAL = False
+NO_GP = (0,)
+MVO = 64
 
 
 def tile_freedamasker_t_kernel(tc, image_feat, proto_emb, out_0, out_1):
@@ -27,7 +27,7 @@ def tile_freedamasker_t_kernel(tc, image_feat, proto_emb, out_0, out_1):
         keep = ctx.enter_context(tc.tile_pool(name="keep", bufs=1))
         small = ctx.enter_context(tc.tile_pool(name="small", bufs=8))
         work = ctx.enter_context(tc.tile_pool(name="work", bufs=2))
-        grpool = ctx.enter_context(tc.tile_pool(name="grpool", bufs=2))
+        grpool = ctx.enter_context(tc.tile_pool(name="grpool", bufs=1))
         ps_xt = ctx.enter_context(tc.psum_pool(name="ps_xt", bufs=3))
         ps_r = ctx.enter_context(tc.psum_pool(name="ps_r", bufs=3))
         ps_o = ctx.enter_context(tc.psum_pool(name="ps_o", bufs=2))
@@ -39,7 +39,7 @@ def tile_freedamasker_t_kernel(tc, image_feat, proto_emb, out_0, out_1):
             xb = keep.tile([P, 4, 1024], BF16, name="x%d" % b)
             src = image_feat[b].rearrange("(p t) h w -> p t (h w)", t=4)
             if b == 0:
-                for lo, hi in ((0, 256), (256, 512), (512, 1024)):
+                for lo, hi in ((512, 768), (768, 1024), (0, 512)):
                     nc.sync.dma_start(out=xb[:, :, lo:hi], in_=src[:, :, lo:hi])
             else:
                 nc.sync.dma_start(out=xb[:], in_=src)
@@ -97,114 +97,119 @@ def tile_freedamasker_t_kernel(tc, image_feat, proto_emb, out_0, out_1):
         grps = {}
         cds = {}
         outs = {}
+        seq = [(b, u) for b in range(NB) for u in (2, 3, 0, 1)]
 
-        def t1(g):
-            b, half = divmod(g, 2)
+        def mvo(b):
+            return 256 if b in NO_GP else MVO
+
+        def t1(k):
+            b, u = seq[k]
             xw = xs[b][:].bitcast(F32)
-            banks = []
-            for k in range(2):
-                xt = ps_xt.tile([P, 512], F32, name="xt")
-                w0 = 256 * half + 128 * k
-                for t in range(4):
-                    nc.tensor.transpose(
-                        xt[:, 128 * t:128 * (t + 1)], xw[:, t, w0:w0 + 128], ident_f[:]
-                    )
-                banks.append(xt)
-            xts[g] = banks
-            sss[g] = small.tile([P, 4], F32, name="ss")
+            xt = ps_xt.tile([P, 512], F32, name="xt")
+            for t in range(4):
+                nc.tensor.transpose(
+                    xt[:, 128 * t:128 * (t + 1)], xw[:, t, 128 * u:128 * (u + 1)], ident_f[:]
+                )
+            xts[k] = xt
 
-        def sumsq(g, k):
-            v = xts[g][k][:].bitcast(BF16).rearrange("p (c e) -> p c e", e=2)
+        def sumsq(k):
+            b, u = seq[k]
+            h, j = divmod(u, 2)
+            if j == 0:
+                sss[(b, h)] = small.tile([P, 4], F32, name="ss")
+            v = xts[k][:].bitcast(BF16).rearrange("p (c e) -> p c e", e=2)
             for e in range(2):
                 junk = work.tile([P, 512], BF16, name="junk")
                 nc.scalar.activation(
                     out=junk[:], in_=v[:, :, e], func=ACT.Square,
-                    accum_out=sss[g][:, 2 * k + e:2 * k + e + 1],
+                    accum_out=sss[(b, h)][:, 2 * j + e:2 * j + e + 1],
                 )
 
-        def root(g):
+        def root(b, h):
             nrm = small.tile([P, 4], F32, name="nrm")
-            nc.scalar.activation(out=nrm[:], in_=sss[g][:], func=ACT.Sqrt, bias=eps[:, 0:1])
-            nrms[g] = nrm
+            nc.scalar.activation(out=nrm[:], in_=sss[(b, h)][:], func=ACT.Sqrt, bias=eps[:, 0:1])
+            nrms[(b, h)] = nrm
 
-        def recip(g):
+        def recip(b, h):
             rin = small.tile([P, 4], F32, name="rin")
-            nc.vector.reciprocal(out=rin[:], in_=nrms[g][:])
-            rins[g] = rin
+            nc.vector.reciprocal(out=rin[:], in_=nrms[(b, h)][:])
+            rins[(b, h)] = rin
 
-        def bcast_t(g):
+        def bcast_t(b, h):
             rp = ps_r.tile([P, 2, 256], F32, name="rp")
-            for k in range(2):
+            for j in range(2):
                 for e in range(2):
-                    c = 2 * k + e
+                    c = 2 * j + e
                     nc.tensor.transpose(
-                        rp[:, e, 128 * k:128 * (k + 1)],
-                        rins[g][:, c:c + 1].to_broadcast([P, P]), ident_f[:],
+                        rp[:, e, 128 * j:128 * (j + 1)],
+                        rins[(b, h)][:, c:c + 1].to_broadcast([P, P]), ident_f[:],
                     )
-            rbs[g] = rp
+            rbs[(b, h)] = rp
 
-        def rcopy(g):
-            if MV < 256:
-                rs = work.tile([P, 256 - MV, 2], F32, name="rs")
-                nc.scalar.copy(out=rs[:], in_=rbs[g][:, :, MV:256].rearrange("p e m -> p m e"))
-                rss[g] = rs
+        def rcopy(b):
+            mv = mvo(b)
+            if mv < 256:
+                rs = work.tile([P, 256 - mv, 2], F32, name="rs")
+                nc.scalar.copy(out=rs[:], in_=rbs[(b, 1)][:, :, mv:256].rearrange("p e m -> p m e"))
+                rss[b] = rs
 
-        def scale_g(g):
-            b, half = divmod(g, 2)
-            grp = grpool.tile([P, 2048], BF16, name="grp", align_bytes=64)
-            grps[g] = grp
-            w0 = 512 * half
-            if MV < 256:
-                nw = 2 * (256 - MV)
+        def scale_g(b):
+            mv = mvo(b)
+            grp = grpool.tile([P, 4096], BF16, name="grp", align_bytes=64)
+            grps[b] = grp
+            if mv < 256:
+                nw = 2 * (256 - mv)
                 nc.gpsimd.tensor_tensor(
-                    out=grp[:, 8 * MV:2048].rearrange("p (w t) -> p w t", t=4),
-                    in0=xs[b][:, :, w0 + 2 * MV:w0 + 512].rearrange("p t w -> p w t"),
-                    in1=rss[g][:].rearrange("p m e -> p (m e)").unsqueeze(2).to_broadcast([P, nw, 4]),
+                    out=grp[:, 2048 + 8 * mv:4096].rearrange("p (w t) -> p w t", t=4),
+                    in0=xs[b][:, :, 512 + 2 * mv:1024].rearrange("p t w -> p w t"),
+                    in1=rss[b][:].rearrange("p m e -> p (m e)").unsqueeze(2).to_broadcast([P, nw, 4]),
                     op=ALU.mult,
                 )
 
-        def scale_v(g):
-            b, half = divmod(g, 2)
-            grp = grps[g]
-            w0 = 512 * half
-            nc.vector.tensor_tensor(
-                out=grp[:, 0:8 * MV].rearrange("p (m e t) -> p m e t", e=2, t=4),
-                in0=xs[b][:, :, w0:w0 + 2 * MV].rearrange("p t (m e) -> p m e t", e=2),
-                in1=rbs[g][:, :, 0:MV].rearrange("p e m -> p m e").unsqueeze(3).to_broadcast([P, MV, 2, 4]),
-                op=ALU.mult,
-            )
+        def scale_v(b):
+            grp = grps[b]
+            for h, mv in ((0, 256), (1, mvo(b))):
+                if mv > 0:
+                    nc.vector.tensor_tensor(
+                        out=grp[:, 2048 * h:2048 * h + 8 * mv].rearrange("p (m e t) -> p m e t", e=2, t=4),
+                        in0=xs[b][:, :, 512 * h:512 * h + 2 * mv].rearrange("p t (m e) -> p m e t", e=2),
+                        in1=rbs[(b, h)][:, :, 0:mv].rearrange("p e m -> p m e")
+                        .unsqueeze(3).to_broadcast([P, mv, 2, 4]),
+                        op=ALU.mult,
+                    )
 
-        def quant(g):
-            codes = work.tile([P, 512], U32, name="codes", align_bytes=64)
-            scl = work.tile([P, 512], U8, name="scl", align_bytes=64)
-            nc.vector.quantize_mx(out=codes[:].bitcast(FP8X4), scales=scl[:], in_=grps[g][:])
-            cds[g] = (codes, scl)
+        def quant(b):
+            codes = work.tile([P, 1024], U32, name="codes", align_bytes=64)
+            scl = work.tile([P, 1024], U8, name="scl", align_bytes=64)
+            nc.vector.quantize_mx(out=codes[:].bitcast(FP8X4), scales=scl[:], in_=grps[b][:])
+            cds[b] = (codes, scl)
 
-        def mx(g):
-            codes, scl = cds[g]
-            o = ps_o.tile([P, 512], F32, name="o")
-            for j in range(4):
-                cols = slice(128 * j, 128 * (j + 1))
-                nc.tensor.matmul_mx(
-                    out=o[:, cols],
-                    lhsT=codes[:, cols].bitcast(FP8X4), lhsT_scale=scl[:, cols],
-                    rhs=pcodes[:].bitcast(FP8X4), rhs_scale=pscl[:],
-                    start=True, stop=True,
+        def mx(b):
+            codes, scl = cds[b]
+            for h in range(2):
+                o = ps_o.tile([P, 512], F32, name="o")
+                for j in range(4):
+                    cols = slice(512 * h + 128 * j, 512 * h + 128 * (j + 1))
+                    nc.tensor.matmul_mx(
+                        out=o[:, 128 * j:128 * (j + 1)],
+                        lhsT=codes[:, cols].bitcast(FP8X4), lhsT_scale=scl[:, cols],
+                        rhs=pcodes[:].bitcast(FP8X4), rhs_scale=pscl[:],
+                        start=True, stop=True,
+                    )
+                outs[(b, h)] = o
+
+        def reduce(b):
+            for h in range(2):
+                ov = outs[(b, h)][:].rearrange("p (j n k) -> p j n k", n=4, k=32)
+                a0 = 4 * h
+                nc.vector.tensor_reduce(
+                    out=res_max_v[:, b, :, a0:a0 + 4].rearrange("p n j -> p j n"),
+                    in_=ov, axis=AX.X, op=ALU.max,
                 )
-            outs[g] = o
-
-        def reduce(g):
-            b, half = divmod(g, 2)
-            ov = outs[g][:].rearrange("p (j n k) -> p j n k", n=4, k=32)
-            a0 = 4 * half
-            nc.vector.tensor_reduce(
-                out=res_max_v[:, b, :, a0:a0 + 4].rearrange("p n j -> p j n"),
-                in_=ov, axis=AX.X, op=ALU.max,
-            )
-            nc.vector.tensor_reduce(
-                out=res_sum_v[:, b, :, a0:a0 + 4].rearrange("p n j -> p j n"),
-                in_=ov, axis=AX.X, op=ALU.add,
-            )
+                nc.vector.tensor_reduce(
+                    out=res_sum_v[:, b, :, a0:a0 + 4].rearrange("p n j -> p j n"),
+                    in_=ov, axis=AX.X, op=ALU.add,
+                )
 
         def mix(q):
             cols = slice(128 * q, 128 * (q + 1))
@@ -220,36 +225,40 @@ def tile_freedamasker_t_kernel(tc, image_feat, proto_emb, out_0, out_1):
             nc.tensor.transpose(fin[:], sim_t[:, cols], ident_f[:])
             return fin
 
-        def ok(g):
-            return 0 <= g < NG
+        def ok(b):
+            return 0 <= b < NB
 
         def body():
-            for i in range(-6, NG):
+            t1(0)
+            t1(1)
+            for i in range(-4, NB):
                 if ok(i):
                     quant(i)
-                if ok(i + 2):
-                    scale_g(i + 2)
                 if ok(i + 1):
+                    scale_g(i + 1)
                     scale_v(i + 1)
-                if ok(i + 3):
-                    bcast_t(i + 3)
-                if ok(i + 5):
-                    sumsq(i + 5, 0)
-                if ok(i + 3):
-                    rcopy(i + 3)
-                if ok(i + 5):
-                    sumsq(i + 5, 1)
-                    root(i + 5)
                 if ok(i):
                     mx(i)
-                if ok(i + 6):
-                    t1(i + 6)
+                if ok(i + 2):
+                    bcast_t(i + 2, 1)
+                    rcopy(i + 2)
+                    bcast_t(i + 2, 0)
+                if ok(i + 4):
+                    for s in range(4):
+                        k = 4 * (i + 4) + s
+                        if k + 2 < len(seq):
+                            t1(k + 2)
+                        sumsq(k)
+                        if s == 1:
+                            root(i + 4, 1)
+                    root(i + 4, 0)
                 if ok(i):
                     reduce(i)
-                if ok(i + 4):
-                    recip(i + 4)
-                if ok(i) and i % 8 == 7 and i < NG - 1:
-                    q = i // 8
+                if ok(i + 3):
+                    recip(i + 3, 1)
+                    recip(i + 3, 0)
+                if ok(i) and i % 4 == 3 and i < NB - 1:
+                    q = i // 4
                     fin = mix(q)
                     nc.scalar.copy(out=sim_sb[:, 128 * q:128 * (q + 1)], in_=fin[:])
                     nc.sync.dma_start(out=dst1[:, q, :], in_=sim_sb[:, 128 * q:128 * (q + 1)])

@@ -17,8 +17,10 @@ AX = mybir.AxisListType
 P = 128
 NB = 16
 MANUAL = False
-NO_GP = (0,)
-MVO = 64
+DS = (2, 5, 8, 11, 12, 13, 14, 15)
+MV_FIRST = 160
+MV_DS = 114
+MVO = 86
 
 
 def tile_freedamasker_t_kernel(tc, image_feat, proto_emb, out_0, out_1):
@@ -100,7 +102,9 @@ def tile_freedamasker_t_kernel(tc, image_feat, proto_emb, out_0, out_1):
         seq = [(b, u) for b in range(NB) for u in (2, 3, 0, 1)]
 
         def mvo(b):
-            return 256 if b in NO_GP else MVO
+            if b == 0:
+                return MV_FIRST
+            return MV_DS if (b - 1) in DS else MVO
 
         def t1(k):
             b, u = seq[k]
@@ -206,10 +210,19 @@ def tile_freedamasker_t_kernel(tc, image_feat, proto_emb, out_0, out_1):
                     out=res_max_v[:, b, :, a0:a0 + 4].rearrange("p n j -> p j n"),
                     in_=ov, axis=AX.X, op=ALU.max,
                 )
-                nc.vector.tensor_reduce(
-                    out=res_sum_v[:, b, :, a0:a0 + 4].rearrange("p n j -> p j n"),
-                    in_=ov, axis=AX.X, op=ALU.add,
-                )
+                if b in DS:
+                    for j in range(4):
+                        for n in range(4):
+                            sj = work.tile([P, 32], F32, name="sj")
+                            nc.scalar.activation(
+                                out=sj[:], in_=ov[:, j, n, :], func=ACT.Copy,
+                                accum_out=res_sum_v[:, b, n, a0 + j:a0 + j + 1],
+                            )
+                else:
+                    nc.vector.tensor_reduce(
+                        out=res_sum_v[:, b, :, a0:a0 + 4].rearrange("p n j -> p j n"),
+                        in_=ov, axis=AX.X, op=ALU.add,
+                    )
 
         def mix(q):
             cols = slice(128 * q, 128 * (q + 1))

@@ -16,11 +16,8 @@ AX = mybir.AxisListType
 
 P = 128
 NB = 16
-MANUAL = False
-DS = (2, 5, 8, 11, 12, 13, 14, 15)
-MV_FIRST = 160
-MV_DS = 114
-MVO = 86
+GP = 192
+BN_HEAD = 1
 
 
 def tile_freedamasker_t_kernel(tc, image_feat, proto_emb, out_0, out_1):
@@ -99,129 +96,151 @@ def tile_freedamasker_t_kernel(tc, image_feat, proto_emb, out_0, out_1):
         grps = {}
         cds = {}
         outs = {}
-        seq = [(b, u) for b in range(NB) for u in (2, 3, 0, 1)]
+        rounds = [(0, 512, 512, 0, 0), (0, 0, 512, 0, BN_HEAD)]
+        rounds += [(b, 0, 1024, GP, 0) for b in range(1, NB - 1)]
+        rounds += [(NB - 1, 512, 512, 0, 0), (NB - 1, 0, 256, 0, 0), (NB - 1, 256, 256, 0, 0)]
+        NR = len(rounds)
 
-        def mvo(b):
-            if b == 0:
-                return MV_FIRST
-            return MV_DS if (b - 1) in DS else MVO
+        def segs(r):
+            npx = rounds[r][2]
+            return [(s, min(512, npx - 512 * s)) for s in range((npx + 511) // 512)]
+
+        seq = []
+        for r in range(NR):
+            for s, spx in reversed(segs(r)):
+                for j in range(spx // 256):
+                    seq.append((r, s, j))
 
         def t1(k):
-            b, u = seq[k]
+            r, s, j = seq[k]
+            b, lo = rounds[r][0], rounds[r][1]
             xw = xs[b][:].bitcast(F32)
+            w0 = (lo + 512 * s + 256 * j) // 2
             xt = ps_xt.tile([P, 512], F32, name="xt")
             for t in range(4):
                 nc.tensor.transpose(
-                    xt[:, 128 * t:128 * (t + 1)], xw[:, t, 128 * u:128 * (u + 1)], ident_f[:]
+                    xt[:, 128 * t:128 * (t + 1)], xw[:, t, w0:w0 + 128], ident_f[:]
                 )
             xts[k] = xt
 
         def sumsq(k):
-            b, u = seq[k]
-            h, j = divmod(u, 2)
-            if j == 0:
-                sss[(b, h)] = small.tile([P, 4], F32, name="ss")
-            v = xts[k][:].bitcast(BF16).rearrange("p (c e) -> p c e", e=2)
-            for e in range(2):
-                junk = work.tile([P, 512], BF16, name="junk")
-                nc.scalar.activation(
-                    out=junk[:], in_=v[:, :, e], func=ACT.Square,
-                    accum_out=sss[(b, h)][:, 2 * j + e:2 * j + e + 1],
+            r, s, j = seq[k]
+            if r not in sss:
+                sss[r] = small.tile([P, 8], F32, name="ss")
+            c0 = 4 * s + 2 * j
+            xb16 = xts[k][:].bitcast(BF16)
+            if rounds[r][4] == 1:
+                st = small.tile([P, 2, 6], F32, name="st")
+                for h in range(2):
+                    nc.vector.bn_stats(out=st[:, h, :], in_=xb16[:, 512 * h:512 * (h + 1)])
+                sv = st[:].rearrange("p h (e s) -> p h e s", s=3)
+                sq = small.tile([P, 2, 2], F32, name="sq")
+                nc.vector.tensor_tensor(out=sq[:], in0=sv[:, :, :, 1], in1=sv[:, :, :, 1], op=ALU.mult)
+                tot = small.tile([P, 2, 2], F32, name="tot")
+                nc.vector.scalar_tensor_tensor(
+                    out=tot[:], in0=sq[:], scalar=256.0, in1=sv[:, :, :, 2], op0=ALU.mult, op1=ALU.add
                 )
-
-        def root(b, h):
-            nrm = small.tile([P, 4], F32, name="nrm")
-            nc.scalar.activation(out=nrm[:], in_=sss[(b, h)][:], func=ACT.Sqrt, bias=eps[:, 0:1])
-            nrms[(b, h)] = nrm
-
-        def recip(b, h):
-            rin = small.tile([P, 4], F32, name="rin")
-            nc.vector.reciprocal(out=rin[:], in_=nrms[(b, h)][:])
-            rins[(b, h)] = rin
-
-        def bcast_t(b, h):
-            rp = ps_r.tile([P, 2, 256], F32, name="rp")
-            for j in range(2):
+                nc.vector.tensor_tensor(
+                    out=sss[r][:, c0:c0 + 2], in0=tot[:, 0, :], in1=tot[:, 1, :], op=ALU.add
+                )
+            else:
+                v = xb16.rearrange("p (c e) -> p c e", e=2)
                 for e in range(2):
-                    c = 2 * j + e
+                    junk = work.tile([P, 512], BF16, name="junk")
+                    nc.scalar.activation(
+                        out=junk[:], in_=v[:, :, e], func=ACT.Square,
+                        accum_out=sss[r][:, c0 + e:c0 + e + 1],
+                    )
+
+        def root(r):
+            nco = rounds[r][2] // 128
+            nrm = small.tile([P, 8], F32, name="nrm")
+            nc.scalar.activation(
+                out=nrm[:, 0:nco], in_=sss[r][:, 0:nco], func=ACT.Sqrt, bias=eps[:, 0:1]
+            )
+            nrms[r] = nrm
+
+        def recip(r):
+            nco = rounds[r][2] // 128
+            rin = small.tile([P, 8], F32, name="rin")
+            nc.vector.reciprocal(out=rin[:, 0:nco], in_=nrms[r][:, 0:nco])
+            rins[r] = rin
+
+        def bcast_t(r, s, spx):
+            rp = ps_r.tile([P, 2, 256], F32, name="rp")
+            for j in range(spx // 256):
+                for e in range(2):
+                    c = 4 * s + 2 * j + e
                     nc.tensor.transpose(
                         rp[:, e, 128 * j:128 * (j + 1)],
-                        rins[(b, h)][:, c:c + 1].to_broadcast([P, P]), ident_f[:],
+                        rins[r][:, c:c + 1].to_broadcast([P, P]), ident_f[:],
                     )
-            rbs[(b, h)] = rp
+            rbs[(r, s)] = rp
 
-        def rcopy(b):
-            mv = mvo(b)
-            if mv < 256:
-                rs = work.tile([P, 256 - mv, 2], F32, name="rs")
-                nc.scalar.copy(out=rs[:], in_=rbs[(b, 1)][:, :, mv:256].rearrange("p e m -> p m e"))
-                rss[b] = rs
+        def spread(r):
+            gp = rounds[r][3]
+            for s, spx in reversed(segs(r)):
+                bcast_t(r, s, spx)
+                if gp > 0 and s == 1:
+                    rs = work.tile([P, gp, 2], F32, name="rs")
+                    nc.scalar.copy(
+                        out=rs[:], in_=rbs[(r, 1)][:, :, 256 - gp:256].rearrange("p e m -> p m e")
+                    )
+                    rss[r] = rs
 
-        def scale_g(b):
-            mv = mvo(b)
-            grp = grpool.tile([P, 4096], BF16, name="grp", align_bytes=64)
-            grps[b] = grp
-            if mv < 256:
-                nw = 2 * (256 - mv)
+        def scale(r):
+            b, lo, npx, gp = rounds[r][0:4]
+            grp = grpool.tile([P, 4 * npx], BF16, name="grp", align_bytes=64)
+            grps[r] = grp
+            if gp > 0:
                 nc.gpsimd.tensor_tensor(
-                    out=grp[:, 2048 + 8 * mv:4096].rearrange("p (w t) -> p w t", t=4),
-                    in0=xs[b][:, :, 512 + 2 * mv:1024].rearrange("p t w -> p w t"),
-                    in1=rss[b][:].rearrange("p m e -> p (m e)").unsqueeze(2).to_broadcast([P, nw, 4]),
+                    out=grp[:, 4096 - 8 * gp:4096].rearrange("p (w t) -> p w t", t=4),
+                    in0=xs[b][:, :, lo + 1024 - 2 * gp:lo + 1024].rearrange("p t w -> p w t"),
+                    in1=rss[r][:].rearrange("p m e -> p (m e)").unsqueeze(2).to_broadcast([P, 2 * gp, 4]),
+                    op=ALU.mult,
+                )
+            for s, spx in reversed(segs(r)):
+                mv = spx // 2 - (gp if s == 1 else 0)
+                x0 = lo + 512 * s
+                nc.vector.tensor_tensor(
+                    out=grp[:, 2048 * s:2048 * s + 8 * mv].rearrange("p (m e t) -> p m e t", e=2, t=4),
+                    in0=xs[b][:, :, x0:x0 + 2 * mv].rearrange("p t (m e) -> p m e t", e=2),
+                    in1=rbs[(r, s)][:, :, 0:mv].rearrange("p e m -> p m e")
+                    .unsqueeze(3).to_broadcast([P, mv, 2, 4]),
                     op=ALU.mult,
                 )
 
-        def scale_v(b):
-            grp = grps[b]
-            for h, mv in ((0, 256), (1, mvo(b))):
-                if mv > 0:
-                    nc.vector.tensor_tensor(
-                        out=grp[:, 2048 * h:2048 * h + 8 * mv].rearrange("p (m e t) -> p m e t", e=2, t=4),
-                        in0=xs[b][:, :, 512 * h:512 * h + 2 * mv].rearrange("p t (m e) -> p m e t", e=2),
-                        in1=rbs[(b, h)][:, :, 0:mv].rearrange("p e m -> p m e")
-                        .unsqueeze(3).to_broadcast([P, mv, 2, 4]),
-                        op=ALU.mult,
-                    )
+        def quant(r):
+            npx = rounds[r][2]
+            codes = work.tile([P, npx], U32, name="codes", align_bytes=64)
+            scl = work.tile([P, npx], U8, name="scl", align_bytes=64)
+            nc.vector.quantize_mx(out=codes[:].bitcast(FP8X4), scales=scl[:], in_=grps[r][:])
+            cds[r] = (codes, scl)
 
-        def quant(b):
-            codes = work.tile([P, 1024], U32, name="codes", align_bytes=64)
-            scl = work.tile([P, 1024], U8, name="scl", align_bytes=64)
-            nc.vector.quantize_mx(out=codes[:].bitcast(FP8X4), scales=scl[:], in_=grps[b][:])
-            cds[b] = (codes, scl)
-
-        def mx(b):
-            codes, scl = cds[b]
-            for h in range(2):
+        def mx(r):
+            codes, scl = cds[r]
+            for s, spx in segs(r):
                 o = ps_o.tile([P, 512], F32, name="o")
-                for j in range(4):
-                    cols = slice(512 * h + 128 * j, 512 * h + 128 * (j + 1))
+                for j in range(spx // 128):
+                    cols = slice(512 * s + 128 * j, 512 * s + 128 * (j + 1))
                     nc.tensor.matmul_mx(
                         out=o[:, 128 * j:128 * (j + 1)],
                         lhsT=codes[:, cols].bitcast(FP8X4), lhsT_scale=scl[:, cols],
                         rhs=pcodes[:].bitcast(FP8X4), rhs_scale=pscl[:],
                         start=True, stop=True,
                     )
-                outs[(b, h)] = o
+                outs[(r, s)] = o
 
-        def reduce(b):
-            for h in range(2):
-                ov = outs[(b, h)][:].rearrange("p (j n k) -> p j n k", n=4, k=32)
-                a0 = 4 * h
-                nc.vector.tensor_reduce(
-                    out=res_max_v[:, b, :, a0:a0 + 4].rearrange("p n j -> p j n"),
-                    in_=ov, axis=AX.X, op=ALU.max,
-                )
-                if b in DS:
-                    for j in range(4):
-                        for n in range(4):
-                            sj = work.tile([P, 32], F32, name="sj")
-                            nc.scalar.activation(
-                                out=sj[:], in_=ov[:, j, n, :], func=ACT.Copy,
-                                accum_out=res_sum_v[:, b, n, a0 + j:a0 + j + 1],
-                            )
-                else:
+        def reduce(r):
+            b, lo = rounds[r][0], rounds[r][1]
+            for s, spx in segs(r):
+                nt = spx // 128
+                ov = outs[(r, s)][:, 0:128 * nt].rearrange("p (j n k) -> p j n k", n=4, k=32)
+                a0 = (lo + 512 * s) // 128
+                for res_v, op in ((res_max_v, ALU.max), (res_sum_v, ALU.add)):
                     nc.vector.tensor_reduce(
-                        out=res_sum_v[:, b, :, a0:a0 + 4].rearrange("p n j -> p j n"),
-                        in_=ov, axis=AX.X, op=ALU.add,
+                        out=res_v[:, b, :, a0:a0 + nt].rearrange("p n j -> p j n"),
+                        in_=ov, axis=AX.X, op=op,
                     )
 
         def mix(q):
@@ -238,49 +257,37 @@ def tile_freedamasker_t_kernel(tc, image_feat, proto_emb, out_0, out_1):
             nc.tensor.transpose(fin[:], sim_t[:, cols], ident_f[:])
             return fin
 
-        def ok(b):
-            return 0 <= b < NB
+        def ok(r):
+            return 0 <= r < NR
 
-        def body():
-            t1(0)
-            t1(1)
-            for i in range(-4, NB):
-                if ok(i):
-                    quant(i)
-                if ok(i + 1):
-                    scale_g(i + 1)
-                    scale_v(i + 1)
-                if ok(i):
-                    mx(i)
-                if ok(i + 2):
-                    bcast_t(i + 2, 1)
-                    rcopy(i + 2)
-                    bcast_t(i + 2, 0)
-                if ok(i + 4):
-                    for s in range(4):
-                        k = 4 * (i + 4) + s
-                        if k + 2 < len(seq):
-                            t1(k + 2)
-                        sumsq(k)
-                        if s == 1:
-                            root(i + 4, 1)
-                    root(i + 4, 0)
-                if ok(i):
-                    reduce(i)
-                if ok(i + 3):
-                    recip(i + 3, 1)
-                    recip(i + 3, 0)
-                if ok(i) and i % 4 == 3 and i < NB - 1:
-                    q = i // 4
-                    fin = mix(q)
-                    nc.scalar.copy(out=sim_sb[:, 128 * q:128 * (q + 1)], in_=fin[:])
-                    nc.sync.dma_start(out=dst1[:, q, :], in_=sim_sb[:, 128 * q:128 * (q + 1)])
-
-        if MANUAL:
-            with tc.manual_schedule():
-                body()
-        else:
-            body()
+        t1(0)
+        t1(1)
+        done = 0
+        for i in range(-4, NR):
+            if ok(i):
+                quant(i)
+            if ok(i + 1):
+                scale(i + 1)
+            if ok(i):
+                mx(i)
+            if ok(i + 2):
+                spread(i + 2)
+            if ok(i + 4):
+                while done < len(seq) and seq[done][0] == i + 4:
+                    if done + 2 < len(seq):
+                        t1(done + 2)
+                    sumsq(done)
+                    done += 1
+                root(i + 4)
+            if ok(i):
+                reduce(i)
+            if ok(i + 3):
+                recip(i + 3)
+            if ok(i) and rounds[i][0] % 4 == 3 and rounds[i][0] < NB - 1:
+                q = rounds[i][0] // 4
+                fin = mix(q)
+                nc.vector.tensor_copy(out=sim_sb[:, 128 * q:128 * (q + 1)], in_=fin[:])
+                nc.sync.dma_start(out=dst1[:, q, :], in_=sim_sb[:, 128 * q:128 * (q + 1)])
 
         nc.scalar.activation(out=mask_sb[:, 0:384], in_=sim_sb[:, 0:384], func=ACT.Sigmoid)
         nc.sync.dma_start(

@@ -16,8 +16,9 @@ AX = mybir.AxisListType
 
 P = 128
 NB = 16
-GP = 192
-BN_HEAD = 1
+MANUAL = False
+NO_GP = (0,)
+MVO = 88
 
 
 def tile_freedamasker_t_kernel(tc, image_feat, proto_emb, out_0, out_1):
@@ -96,152 +97,119 @@ def tile_freedamasker_t_kernel(tc, image_feat, proto_emb, out_0, out_1):
         grps = {}
         cds = {}
         outs = {}
-        rounds = [(0, 512, 512, 0, 0), (0, 0, 512, 0, BN_HEAD)]
-        rounds += [(b, 0, 1024, GP, 0) for b in range(1, NB - 1)]
-        rounds += [(NB - 1, 512, 512, 0, 0), (NB - 1, 0, 256, 0, 0), (NB - 1, 256, 256, 0, 0)]
-        NR = len(rounds)
+        seq = [(b, u) for b in range(NB) for u in (2, 3, 0, 1)]
 
-        def segs(r):
-            npx = rounds[r][2]
-            return [(s, min(512, npx - 512 * s)) for s in range((npx + 511) // 512)]
-
-        seq = []
-        for r in range(NR):
-            for s, spx in reversed(segs(r)):
-                for j in range(spx // 256):
-                    seq.append((r, s, j))
+        def mvo(b):
+            return 256 if b in NO_GP else MVO
 
         def t1(k):
-            r, s, j = seq[k]
-            b, lo = rounds[r][0], rounds[r][1]
+            b, u = seq[k]
             xw = xs[b][:].bitcast(F32)
-            w0 = (lo + 512 * s + 256 * j) // 2
             xt = ps_xt.tile([P, 512], F32, name="xt")
             for t in range(4):
                 nc.tensor.transpose(
-                    xt[:, 128 * t:128 * (t + 1)], xw[:, t, w0:w0 + 128], ident_f[:]
+                    xt[:, 128 * t:128 * (t + 1)], xw[:, t, 128 * u:128 * (u + 1)], ident_f[:]
                 )
             xts[k] = xt
 
         def sumsq(k):
-            r, s, j = seq[k]
-            if r not in sss:
-                sss[r] = small.tile([P, 8], F32, name="ss")
-            c0 = 4 * s + 2 * j
-            xb16 = xts[k][:].bitcast(BF16)
-            if rounds[r][4] == 1:
-                st = small.tile([P, 2, 6], F32, name="st")
-                for h in range(2):
-                    nc.vector.bn_stats(out=st[:, h, :], in_=xb16[:, 512 * h:512 * (h + 1)])
-                sv = st[:].rearrange("p h (e s) -> p h e s", s=3)
-                sq = small.tile([P, 2, 2], F32, name="sq")
-                nc.vector.tensor_tensor(out=sq[:], in0=sv[:, :, :, 1], in1=sv[:, :, :, 1], op=ALU.mult)
-                tot = small.tile([P, 2, 2], F32, name="tot")
-                nc.vector.scalar_tensor_tensor(
-                    out=tot[:], in0=sq[:], scalar=256.0, in1=sv[:, :, :, 2], op0=ALU.mult, op1=ALU.add
+            b, u = seq[k]
+            h, j = divmod(u, 2)
+            if j == 0:
+                sss[(b, h)] = small.tile([P, 4], F32, name="ss")
+            v = xts[k][:].bitcast(BF16).rearrange("p (c e) -> p c e", e=2)
+            for e in range(2):
+                junk = work.tile([P, 512], BF16, name="junk")
+                nc.scalar.activation(
+                    out=junk[:], in_=v[:, :, e], func=ACT.Square,
+                    accum_out=sss[(b, h)][:, 2 * j + e:2 * j + e + 1],
                 )
-                nc.vector.tensor_tensor(
-                    out=sss[r][:, c0:c0 + 2], in0=tot[:, 0, :], in1=tot[:, 1, :], op=ALU.add
-                )
-            else:
-                v = xb16.rearrange("p (c e) -> p c e", e=2)
-                for e in range(2):
-                    junk = work.tile([P, 512], BF16, name="junk")
-                    nc.scalar.activation(
-                        out=junk[:], in_=v[:, :, e], func=ACT.Square,
-                        accum_out=sss[r][:, c0 + e:c0 + e + 1],
-                    )
 
-        def root(r):
-            nco = rounds[r][2] // 128
-            nrm = small.tile([P, 8], F32, name="nrm")
-            nc.scalar.activation(
-                out=nrm[:, 0:nco], in_=sss[r][:, 0:nco], func=ACT.Sqrt, bias=eps[:, 0:1]
-            )
-            nrms[r] = nrm
+        def root(b, h):
+            nrm = small.tile([P, 4], F32, name="nrm")
+            nc.scalar.activation(out=nrm[:], in_=sss[(b, h)][:], func=ACT.Sqrt, bias=eps[:, 0:1])
+            nrms[(b, h)] = nrm
 
-        def recip(r):
-            nco = rounds[r][2] // 128
-            rin = small.tile([P, 8], F32, name="rin")
-            nc.vector.reciprocal(out=rin[:, 0:nco], in_=nrms[r][:, 0:nco])
-            rins[r] = rin
+        def recip(b, h):
+            rin = small.tile([P, 4], F32, name="rin")
+            nc.vector.reciprocal(out=rin[:], in_=nrms[(b, h)][:])
+            rins[(b, h)] = rin
 
-        def bcast_t(r, s, spx):
+        def bcast_t(b, h):
             rp = ps_r.tile([P, 2, 256], F32, name="rp")
-            for j in range(spx // 256):
+            for j in range(2):
                 for e in range(2):
-                    c = 4 * s + 2 * j + e
+                    c = 2 * j + e
                     nc.tensor.transpose(
                         rp[:, e, 128 * j:128 * (j + 1)],
-                        rins[r][:, c:c + 1].to_broadcast([P, P]), ident_f[:],
+                        rins[(b, h)][:, c:c + 1].to_broadcast([P, P]), ident_f[:],
                     )
-            rbs[(r, s)] = rp
+            rbs[(b, h)] = rp
 
-        def spread(r):
-            gp = rounds[r][3]
-            for s, spx in reversed(segs(r)):
-                bcast_t(r, s, spx)
-                if gp > 0 and s == 1:
-                    rs = work.tile([P, gp, 2], F32, name="rs")
-                    nc.scalar.copy(
-                        out=rs[:], in_=rbs[(r, 1)][:, :, 256 - gp:256].rearrange("p e m -> p m e")
-                    )
-                    rss[r] = rs
+        def rcopy(b):
+            mv = mvo(b)
+            if mv < 256:
+                rs = work.tile([P, 256 - mv, 2], F32, name="rs")
+                nc.scalar.copy(out=rs[:], in_=rbs[(b, 1)][:, :, mv:256].rearrange("p e m -> p m e"))
+                rss[b] = rs
 
-        def scale(r):
-            b, lo, npx, gp = rounds[r][0:4]
-            grp = grpool.tile([P, 4 * npx], BF16, name="grp", align_bytes=64)
-            grps[r] = grp
-            if gp > 0:
+        def scale_g(b):
+            mv = mvo(b)
+            grp = grpool.tile([P, 4096], BF16, name="grp", align_bytes=64)
+            grps[b] = grp
+            if mv < 256:
+                nw = 2 * (256 - mv)
                 nc.gpsimd.tensor_tensor(
-                    out=grp[:, 4096 - 8 * gp:4096].rearrange("p (w t) -> p w t", t=4),
-                    in0=xs[b][:, :, lo + 1024 - 2 * gp:lo + 1024].rearrange("p t w -> p w t"),
-                    in1=rss[r][:].rearrange("p m e -> p (m e)").unsqueeze(2).to_broadcast([P, 2 * gp, 4]),
-                    op=ALU.mult,
-                )
-            for s, spx in reversed(segs(r)):
-                mv = spx // 2 - (gp if s == 1 else 0)
-                x0 = lo + 512 * s
-                nc.vector.tensor_tensor(
-                    out=grp[:, 2048 * s:2048 * s + 8 * mv].rearrange("p (m e t) -> p m e t", e=2, t=4),
-                    in0=xs[b][:, :, x0:x0 + 2 * mv].rearrange("p t (m e) -> p m e t", e=2),
-                    in1=rbs[(r, s)][:, :, 0:mv].rearrange("p e m -> p m e")
-                    .unsqueeze(3).to_broadcast([P, mv, 2, 4]),
+                    out=grp[:, 2048 + 8 * mv:4096].rearrange("p (w t) -> p w t", t=4),
+                    in0=xs[b][:, :, 512 + 2 * mv:1024].rearrange("p t w -> p w t"),
+                    in1=rss[b][:].rearrange("p m e -> p (m e)").unsqueeze(2).to_broadcast([P, nw, 4]),
                     op=ALU.mult,
                 )
 
-        def quant(r):
-            npx = rounds[r][2]
-            codes = work.tile([P, npx], U32, name="codes", align_bytes=64)
-            scl = work.tile([P, npx], U8, name="scl", align_bytes=64)
-            nc.vector.quantize_mx(out=codes[:].bitcast(FP8X4), scales=scl[:], in_=grps[r][:])
-            cds[r] = (codes, scl)
+        def scale_v(b):
+            grp = grps[b]
+            for h, mv in ((0, 256), (1, mvo(b))):
+                if mv > 0:
+                    nc.vector.tensor_tensor(
+                        out=grp[:, 2048 * h:2048 * h + 8 * mv].rearrange("p (m e t) -> p m e t", e=2, t=4),
+                        in0=xs[b][:, :, 512 * h:512 * h + 2 * mv].rearrange("p t (m e) -> p m e t", e=2),
+                        in1=rbs[(b, h)][:, :, 0:mv].rearrange("p e m -> p m e")
+                        .unsqueeze(3).to_broadcast([P, mv, 2, 4]),
+                        op=ALU.mult,
+                    )
 
-        def mx(r):
-            codes, scl = cds[r]
-            for s, spx in segs(r):
+        def quant(b):
+            codes = work.tile([P, 1024], U32, name="codes", align_bytes=64)
+            scl = work.tile([P, 1024], U8, name="scl", align_bytes=64)
+            nc.vector.quantize_mx(out=codes[:].bitcast(FP8X4), scales=scl[:], in_=grps[b][:])
+            cds[b] = (codes, scl)
+
+        def mx(b):
+            codes, scl = cds[b]
+            for h in range(2):
                 o = ps_o.tile([P, 512], F32, name="o")
-                for j in range(spx // 128):
-                    cols = slice(512 * s + 128 * j, 512 * s + 128 * (j + 1))
+                for j in range(4):
+                    cols = slice(512 * h + 128 * j, 512 * h + 128 * (j + 1))
                     nc.tensor.matmul_mx(
                         out=o[:, 128 * j:128 * (j + 1)],
                         lhsT=codes[:, cols].bitcast(FP8X4), lhsT_scale=scl[:, cols],
                         rhs=pcodes[:].bitcast(FP8X4), rhs_scale=pscl[:],
                         start=True, stop=True,
                     )
-                outs[(r, s)] = o
+                outs[(b, h)] = o
 
-        def reduce(r):
-            b, lo = rounds[r][0], rounds[r][1]
-            for s, spx in segs(r):
-                nt = spx // 128
-                ov = outs[(r, s)][:, 0:128 * nt].rearrange("p (j n k) -> p j n k", n=4, k=32)
-                a0 = (lo + 512 * s) // 128
-                for res_v, op in ((res_max_v, ALU.max), (res_sum_v, ALU.add)):
-                    nc.vector.tensor_reduce(
-                        out=res_v[:, b, :, a0:a0 + nt].rearrange("p n j -> p j n"),
-                        in_=ov, axis=AX.X, op=op,
-                    )
+        def reduce(b):
+            for h in range(2):
+                ov = outs[(b, h)][:].rearrange("p (j n k) -> p j n k", n=4, k=32)
+                a0 = 4 * h
+                nc.vector.tensor_reduce(
+                    out=res_max_v[:, b, :, a0:a0 + 4].rearrange("p n j -> p j n"),
+                    in_=ov, axis=AX.X, op=ALU.max,
+                )
+                nc.vector.tensor_reduce(
+                    out=res_sum_v[:, b, :, a0:a0 + 4].rearrange("p n j -> p j n"),
+                    in_=ov, axis=AX.X, op=ALU.add,
+                )
 
         def mix(q):
             cols = slice(128 * q, 128 * (q + 1))
@@ -257,37 +225,49 @@ def tile_freedamasker_t_kernel(tc, image_feat, proto_emb, out_0, out_1):
             nc.tensor.transpose(fin[:], sim_t[:, cols], ident_f[:])
             return fin
 
-        def ok(r):
-            return 0 <= r < NR
+        def ok(b):
+            return 0 <= b < NB
 
-        t1(0)
-        t1(1)
-        done = 0
-        for i in range(-4, NR):
-            if ok(i):
-                quant(i)
-            if ok(i + 1):
-                scale(i + 1)
-            if ok(i):
-                mx(i)
-            if ok(i + 2):
-                spread(i + 2)
-            if ok(i + 4):
-                while done < len(seq) and seq[done][0] == i + 4:
-                    if done + 2 < len(seq):
-                        t1(done + 2)
-                    sumsq(done)
-                    done += 1
-                root(i + 4)
-            if ok(i):
-                reduce(i)
-            if ok(i + 3):
-                recip(i + 3)
-            if ok(i) and rounds[i][0] % 4 == 3 and rounds[i][0] < NB - 1:
-                q = rounds[i][0] // 4
-                fin = mix(q)
-                nc.vector.tensor_copy(out=sim_sb[:, 128 * q:128 * (q + 1)], in_=fin[:])
-                nc.sync.dma_start(out=dst1[:, q, :], in_=sim_sb[:, 128 * q:128 * (q + 1)])
+        def body():
+            t1(0)
+            t1(1)
+            for i in range(-4, NB):
+                if ok(i):
+                    quant(i)
+                if ok(i + 1):
+                    scale_g(i + 1)
+                    scale_v(i + 1)
+                if ok(i):
+                    mx(i)
+                if ok(i + 2):
+                    bcast_t(i + 2, 1)
+                    rcopy(i + 2)
+                    bcast_t(i + 2, 0)
+                if ok(i + 4):
+                    for s in range(4):
+                        k = 4 * (i + 4) + s
+                        if k + 2 < len(seq):
+                            t1(k + 2)
+                        sumsq(k)
+                        if s == 1:
+                            root(i + 4, 1)
+                    root(i + 4, 0)
+                if ok(i):
+                    reduce(i)
+                if ok(i + 3):
+                    recip(i + 3, 1)
+                    recip(i + 3, 0)
+                if ok(i) and i % 4 == 3 and i < NB - 1:
+                    q = i // 4
+                    fin = mix(q)
+                    nc.scalar.copy(out=sim_sb[:, 128 * q:128 * (q + 1)], in_=fin[:])
+                    nc.sync.dma_start(out=dst1[:, q, :], in_=sim_sb[:, 128 * q:128 * (q + 1)])
+
+        if MANUAL:
+            with tc.manual_schedule():
+                body()
+        else:
+            body()
 
         nc.scalar.activation(out=mask_sb[:, 0:384], in_=sim_sb[:, 0:384], func=ACT.Sigmoid)
         nc.sync.dma_start(

@@ -18,7 +18,7 @@ P = 128
 NB = 16
 MANUAL = False
 NO_GP = (0,)
-MVO = 88
+MVO = 48
 
 
 def tile_freedamasker_t_kernel(tc, image_feat, proto_emb, out_0, out_1):
@@ -171,10 +171,10 @@ def tile_freedamasker_t_kernel(tc, image_feat, proto_emb, out_0, out_1):
             for h, mv in ((0, 256), (1, mvo(b))):
                 if mv > 0:
                     nc.vector.tensor_tensor(
-                        out=grp[:, 2048 * h:2048 * h + 8 * mv].rearrange("p (m e t) -> p m e t", e=2, t=4),
-                        in0=xs[b][:, :, 512 * h:512 * h + 2 * mv].rearrange("p t (m e) -> p m e t", e=2),
+                        out=grp[:, 2048 * h:2048 * h + 8 * mv].rearrange("p (m e t) -> p m t e", e=2, t=4),
+                        in0=xs[b][:, :, 512 * h:512 * h + 2 * mv].rearrange("p t (m e) -> p m t e", e=2),
                         in1=rbs[(b, h)][:, :, 0:mv].rearrange("p e m -> p m e")
-                        .unsqueeze(3).to_broadcast([P, mv, 2, 4]),
+                        .unsqueeze(2).to_broadcast([P, mv, 4, 2]),
                         op=ALU.mult,
                     )
 

@@ -16,7 +16,6 @@ AX = mybir.AxisListType
 
 P = 128
 NB = 16
-MANUAL = False
 NO_GP = (0,)
 MVO = 48
 
@@ -29,8 +28,9 @@ def tile_freedamasker_t_kernel(tc, image_feat, proto_emb, out_0, out_1):
         work = ctx.enter_context(tc.tile_pool(name="work", bufs=2))
         grpool = ctx.enter_context(tc.tile_pool(name="grpool", bufs=1))
         ps_xt = ctx.enter_context(tc.psum_pool(name="ps_xt", bufs=3))
-        ps_r = ctx.enter_context(tc.psum_pool(name="ps_r", bufs=3))
+        ps_r = ctx.enter_context(tc.psum_pool(name="ps_r", bufs=2))
         ps_o = ctx.enter_context(tc.psum_pool(name="ps_o", bufs=2))
+        ps_s = ctx.enter_context(tc.psum_pool(name="ps_s", bufs=1))
 
         pro = keep.tile([P, 512], BF16, name="pro")
         nc.scalar.dma_start(out=pro[:], in_=proto_emb.rearrange("n k c -> (n k) c"))
@@ -79,14 +79,20 @@ def tile_freedamasker_t_kernel(tc, image_feat, proto_emb, out_0, out_1):
         pt_ps = ps_o.tile([P, 4, P], BF16, name="o")
         for t in range(4):
             nc.tensor.transpose(pt_ps[:, t, :], pn[:, t, :], ident_b[:])
-        pgrp = keep.tile([P, P, 4], BF16, name="pgrp", align_bytes=64)
-        nc.vector.tensor_copy(out=pgrp[:], in_=pt_ps[:].rearrange("p t m -> p m t"))
-        pcodes = keep.tile([P, P], U32, name="pcodes", align_bytes=64)
-        pscl = keep.tile([P, P], U8, name="pscl", align_bytes=64)
-        nc.vector.quantize_mx(
-            out=pcodes[:].bitcast(FP8X4), scales=pscl[:],
-            in_=pgrp[:].rearrange("p m t -> p (m t)"),
-        )
+        pgrp = keep.tile([P, 384, 4], BF16, name="pgrp", align_bytes=64)
+        nc.vector.tensor_copy(out=pgrp[:, 256:384, :], in_=pt_ps[:].rearrange("p t m -> p m t"))
+        for d in range(2):
+            nc.vector.tensor_copy(
+                out=pgrp[:, 0:256, :].rearrange("p (s d q) t -> p d s q t", d=2, q=32)[:, d],
+                in_=pt_ps[:].rearrange("p t (q s) -> p s q t", s=4),
+            )
+        pcodes = keep.tile([P, 384], U32, name="pcodes", align_bytes=64)
+        pscl = keep.tile([P, 384], U8, name="pscl", align_bytes=64)
+        for lo, hi in ((256, 384), (0, 256)):
+            nc.vector.quantize_mx(
+                out=pcodes[:, lo:hi].bitcast(FP8X4), scales=pscl[:, lo:hi],
+                in_=pgrp[:, lo:hi, :].rearrange("p m t -> p (m t)"),
+            )
 
         xts = {}
         sss = {}
@@ -97,6 +103,7 @@ def tile_freedamasker_t_kernel(tc, image_feat, proto_emb, out_0, out_1):
         grps = {}
         cds = {}
         outs = {}
+        sums = {}
         seq = [(b, u) for b in range(NB) for u in (2, 3, 0, 1)]
 
         def mvo(b):
@@ -193,10 +200,22 @@ def tile_freedamasker_t_kernel(tc, image_feat, proto_emb, out_0, out_1):
                     nc.tensor.matmul_mx(
                         out=o[:, 128 * j:128 * (j + 1)],
                         lhsT=codes[:, cols].bitcast(FP8X4), lhsT_scale=scl[:, cols],
-                        rhs=pcodes[:].bitcast(FP8X4), rhs_scale=pscl[:],
+                        rhs=pcodes[:, 256:384].bitcast(FP8X4), rhs_scale=pscl[:, 256:384],
                         start=True, stop=True,
                     )
                 outs[(b, h)] = o
+            sm = ps_s.tile([P, 512], F32, name="sm")
+            for j in range(8):
+                cols = slice(128 * j, 128 * (j + 1))
+                for s in range(4):
+                    pc = slice(64 * s, 64 * s + 128)
+                    nc.tensor.matmul_mx(
+                        out=sm[:, 32 * j:32 * j + 128],
+                        lhsT=codes[:, cols].bitcast(FP8X4), lhsT_scale=scl[:, cols],
+                        rhs=pcodes[:, pc].bitcast(FP8X4), rhs_scale=pscl[:, pc],
+                        start=(s == 0), stop=(s == 3),
+                    )
+            sums[b] = sm
 
         def reduce(b):
             for h in range(2):
@@ -206,10 +225,11 @@ def tile_freedamasker_t_kernel(tc, image_feat, proto_emb, out_0, out_1):
                     out=res_max_v[:, b, :, a0:a0 + 4].rearrange("p n j -> p j n"),
                     in_=ov, axis=AX.X, op=ALU.max,
                 )
-                nc.vector.tensor_reduce(
-                    out=res_sum_v[:, b, :, a0:a0 + 4].rearrange("p n j -> p j n"),
-                    in_=ov, axis=AX.X, op=ALU.add,
-                )
+            nc.vector.tensor_reduce(
+                out=res_sum_v[:, b].rearrange("p n j -> p j n"),
+                in_=sums[b][:, 0:256].rearrange("p (j n g) -> p j n g", n=4, g=8),
+                axis=AX.X, op=ALU.add,
+            )
 
         def mix(q):
             cols = slice(128 * q, 128 * (q + 1))
@@ -263,11 +283,7 @@ def tile_freedamasker_t_kernel(tc, image_feat, proto_emb, out_0, out_1):
                     nc.scalar.copy(out=sim_sb[:, 128 * q:128 * (q + 1)], in_=fin[:])
                     nc.sync.dma_start(out=dst1[:, q, :], in_=sim_sb[:, 128 * q:128 * (q + 1)])
 
-        if MANUAL:
-            with tc.manual_schedule():
-                body()
-        else:
-            body()
+        body()
 
         nc.scalar.activation(out=mask_sb[:, 0:384], in_=sim_sb[:, 0:384], func=ACT.Sigmoid)
         nc.sync.dma_start(

@@ -16,7 +16,6 @@ AX = mybir.AxisListType
 
 P = 128
 NB = 16
-NO_GP = (0,)
 MVO = 48
 
 
@@ -28,9 +27,7 @@ def tile_freedamasker_t_kernel(tc, image_feat, proto_emb, out_0, out_1):
         work = ctx.enter_context(tc.tile_pool(name="work", bufs=2))
         grpool = ctx.enter_context(tc.tile_pool(name="grpool", bufs=1))
         ps_xt = ctx.enter_context(tc.psum_pool(name="ps_xt", bufs=3))
-        ps_r = ctx.enter_context(tc.psum_pool(name="ps_r", bufs=2))
-        ps_o = ctx.enter_context(tc.psum_pool(name="ps_o", bufs=2))
-        ps_s = ctx.enter_context(tc.psum_pool(name="ps_s", bufs=1))
+        ps = ctx.enter_context(tc.psum_pool(name="ps", bufs=1))
 
         pro = keep.tile([P, 512], BF16, name="pro")
         nc.scalar.dma_start(out=pro[:], in_=proto_emb.rearrange("n k c -> (n k) c"))
@@ -64,35 +61,41 @@ def tile_freedamasker_t_kernel(tc, image_feat, proto_emb, out_0, out_1):
         dst0 = out_0.rearrange("b n (a r) w -> (b n a) (r w)", a=8).rearrange("(q p) f -> p q f", p=P)
         dst1 = out_1.rearrange("b n (a r) w -> (b n a) (r w)", a=8).rearrange("(q p) f -> p q f", p=P)
 
-        pjunk = keep.tile([P, 512], BF16, name="pjunk")
-        pss = keep.tile([P, 1], F32, name="pss")
-        nc.scalar.activation(out=pjunk[:], in_=pro[:], func=ACT.Square, accum_out=pss[:])
-        pnrm = keep.tile([P, 1], F32, name="pnrm")
-        nc.scalar.activation(out=pnrm[:], in_=pss[:], func=ACT.Sqrt, bias=eps[:, 0:1])
-        prin = keep.tile([P, 1], F32, name="prin")
-        nc.vector.reciprocal(out=prin[:], in_=pnrm[:])
-        pn = keep.tile([P, 4, P], BF16, name="pn")
-        nc.vector.tensor_scalar(
-            out=pn[:], in0=pro[:].rearrange("m (p t) -> m t p", t=4),
-            scalar1=prin[:, 0:1], scalar2=None, op0=ALU.mult,
-        )
-        pt_ps = ps_o.tile([P, 4, P], BF16, name="o")
-        for t in range(4):
-            nc.tensor.transpose(pt_ps[:, t, :], pn[:, t, :], ident_b[:])
-        pgrp = keep.tile([P, 384, 4], BF16, name="pgrp", align_bytes=64)
-        nc.vector.tensor_copy(out=pgrp[:, 256:384, :], in_=pt_ps[:].rearrange("p t m -> p m t"))
-        for d in range(2):
-            nc.vector.tensor_copy(
-                out=pgrp[:, 0:256, :].rearrange("p (s d q) t -> p d s q t", d=2, q=32)[:, d],
-                in_=pt_ps[:].rearrange("p t (q s) -> p s q t", s=4),
-            )
         pcodes = keep.tile([P, 384], U32, name="pcodes", align_bytes=64)
         pscl = keep.tile([P, 384], U8, name="pscl", align_bytes=64)
-        for lo, hi in ((256, 384), (0, 256)):
-            nc.vector.quantize_mx(
-                out=pcodes[:, lo:hi].bitcast(FP8X4), scales=pscl[:, lo:hi],
-                in_=pgrp[:, lo:hi, :].rearrange("p m t -> p (m t)"),
+
+        def prototypes():
+            psq = keep.tile([P, 512], F32, name="psq")
+            pss = keep.tile([P, 1], F32, name="pss")
+            nc.vector.scalar_tensor_tensor(
+                out=psq[:], in0=pro[:], scalar=1.0, in1=pro[:],
+                op0=ALU.mult, op1=ALU.mult, accum_out=pss[:],
             )
+            pnrm = keep.tile([P, 1], F32, name="pnrm")
+            nc.scalar.activation(out=pnrm[:], in_=pss[:], func=ACT.Sqrt, bias=eps[:, 0:1])
+            prin = keep.tile([P, 1], F32, name="prin")
+            nc.vector.reciprocal(out=prin[:], in_=pnrm[:])
+            pn = keep.tile([P, 4, P], BF16, name="pn")
+            nc.vector.tensor_scalar(
+                out=pn[:], in0=pro[:].rearrange("m (p t) -> m t p", t=4),
+                scalar1=prin[:, 0:1], scalar2=None, op0=ALU.mult,
+            )
+            pt_ps = ps.tile([P, 4, P], BF16, name="pt_ps", tag="o0")
+            for t in range(4):
+                nc.tensor.transpose(pt_ps[:, t, :], pn[:, t, :], ident_b[:])
+            pgrp = keep.tile([P, 384, 4], BF16, name="pgrp", align_bytes=64)
+            nc.vector.tensor_copy(out=pgrp[:, 256:384, :], in_=pt_ps[:].rearrange("p t m -> p m t"))
+            for d in range(2):
+                nc.vector.tensor_copy(
+                    out=pgrp[:, 0:256, :].rearrange("p (s d q) t -> p d s q t", d=2, q=32)[:, d],
+                    in_=pt_ps[:].rearrange("p t (q s) -> p s q t", s=4),
+                )
+            for lo, hi in ((256, 384), (0, 256)):
+                nc.vector.quantize_mx(
+                    out=pcodes[:, lo:hi].bitcast(FP8X4), scales=pscl[:, lo:hi],
+                    in_=pgrp[:, lo:hi, :].rearrange("p m t -> p (m t)"),
+                )
+
 
         xts = {}
         sss = {}
@@ -107,7 +110,7 @@ def tile_freedamasker_t_kernel(tc, image_feat, proto_emb, out_0, out_1):
         seq = [(b, u) for b in range(NB) for u in (2, 3, 0, 1)]
 
         def mvo(b):
-            return 256 if b in NO_GP else MVO
+            return 160 if b == 0 else MVO
 
         def t1(k):
             b, u = seq[k]
@@ -143,7 +146,7 @@ def tile_freedamasker_t_kernel(tc, image_feat, proto_emb, out_0, out_1):
             rins[(b, h)] = rin
 
         def bcast_t(b, h):
-            rp = ps_r.tile([P, 2, 256], F32, name="rp")
+            rp = ps.tile([P, 2, 256], F32, name="rp", tag="rp%d" % h)
             for j in range(2):
                 for e in range(2):
                     c = 2 * j + e
@@ -173,17 +176,16 @@ def tile_freedamasker_t_kernel(tc, image_feat, proto_emb, out_0, out_1):
                     op=ALU.mult,
                 )
 
-        def scale_v(b):
+        def scale_v(b, h):
             grp = grps[b]
-            for h, mv in ((0, 256), (1, mvo(b))):
-                if mv > 0:
-                    nc.vector.tensor_tensor(
-                        out=grp[:, 2048 * h:2048 * h + 8 * mv].rearrange("p (m e t) -> p m t e", e=2, t=4),
-                        in0=xs[b][:, :, 512 * h:512 * h + 2 * mv].rearrange("p t (m e) -> p m t e", e=2),
-                        in1=rbs[(b, h)][:, :, 0:mv].rearrange("p e m -> p m e")
-                        .unsqueeze(2).to_broadcast([P, mv, 4, 2]),
-                        op=ALU.mult,
-                    )
+            mv = mvo(b) if h else 256
+            nc.vector.tensor_tensor(
+                out=grp[:, 2048 * h:2048 * h + 8 * mv].rearrange("p (m e t) -> p m t e", e=2, t=4),
+                in0=xs[b][:, :, 512 * h:512 * h + 2 * mv].rearrange("p t (m e) -> p m t e", e=2),
+                in1=rbs[(b, h)][:, :, 0:mv].rearrange("p e m -> p m e")
+                .unsqueeze(2).to_broadcast([P, mv, 4, 2]),
+                op=ALU.mult,
+            )
 
         def quant(b):
             codes = work.tile([P, 1024], U32, name="codes", align_bytes=64)
@@ -191,10 +193,10 @@ def tile_freedamasker_t_kernel(tc, image_feat, proto_emb, out_0, out_1):
             nc.vector.quantize_mx(out=codes[:].bitcast(FP8X4), scales=scl[:], in_=grps[b][:])
             cds[b] = (codes, scl)
 
-        def mx(b):
+        def mx(b, hh):
             codes, scl = cds[b]
-            for h in range(2):
-                o = ps_o.tile([P, 512], F32, name="o")
+            for h in (hh,):
+                o = ps.tile([P, 512], F32, name="o", tag="o%d" % h)
                 for j in range(4):
                     cols = slice(512 * h + 128 * j, 512 * h + 128 * (j + 1))
                     nc.tensor.matmul_mx(
@@ -204,9 +206,12 @@ def tile_freedamasker_t_kernel(tc, image_feat, proto_emb, out_0, out_1):
                         start=True, stop=True,
                     )
                 outs[(b, h)] = o
-            sm = ps_s.tile([P, 512], F32, name="sm")
-            for j in range(8):
-                cols = slice(128 * j, 128 * (j + 1))
+            if hh == 1:
+                sums[b] = ps.tile([P, 512], F32, name="sm", tag="sm")
+            sm = sums[b]
+            for j in range(4 * (1 - hh), 4 * (1 - hh) + 4):
+                c0 = 128 * ((j + 4) % 8)
+                cols = slice(c0, c0 + 128)
                 for s in range(4):
                     pc = slice(64 * s, 64 * s + 128)
                     nc.tensor.matmul_mx(
@@ -215,21 +220,21 @@ def tile_freedamasker_t_kernel(tc, image_feat, proto_emb, out_0, out_1):
                         rhs=pcodes[:, pc].bitcast(FP8X4), rhs_scale=pscl[:, pc],
                         start=(s == 0), stop=(s == 3),
                     )
-            sums[b] = sm
 
         def reduce(b):
-            for h in range(2):
+            for h in (1, 0):
                 ov = outs[(b, h)][:].rearrange("p (j n k) -> p j n k", n=4, k=32)
                 a0 = 4 * h
                 nc.vector.tensor_reduce(
                     out=res_max_v[:, b, :, a0:a0 + 4].rearrange("p n j -> p j n"),
                     in_=ov, axis=AX.X, op=ALU.max,
                 )
-            nc.vector.tensor_reduce(
-                out=res_sum_v[:, b].rearrange("p n j -> p j n"),
-                in_=sums[b][:, 0:256].rearrange("p (j n g) -> p j n g", n=4, g=8),
-                axis=AX.X, op=ALU.add,
-            )
+            for h in (1, 0):
+                nc.vector.tensor_reduce(
+                    out=res_sum_v[:, b, :, 4 * h:4 * h + 4].rearrange("p n j -> p j n"),
+                    in_=sums[b][:, 128 * (1 - h):128 * (2 - h)].rearrange("p (j n g) -> p j n g", n=4, g=8),
+                    axis=AX.X, op=ALU.add,
+                )
 
         def mix(q):
             cols = slice(128 * q, 128 * (q + 1))
@@ -241,49 +246,66 @@ def tile_freedamasker_t_kernel(tc, image_feat, proto_emb, out_0, out_1):
                 out=sim_t[:, cols], in0=res_max[:, cols], scalar=0.5, in1=tmp[:],
                 op0=ALU.mult, op1=ALU.add,
             )
-            fin = ps_o.tile([P, P], F32, name="o")
+            fin = ps_xt.tile([P, P], F32, name="xt")
             nc.tensor.transpose(fin[:], sim_t[:, cols], ident_f[:])
             return fin
 
         def ok(b):
             return 0 <= b < NB
 
-        def body():
+        def out_sim(q):
+            fin = mix(q)
+            nc.scalar.copy(out=sim_sb[:, 128 * q:128 * (q + 1)], in_=fin[:])
+            nc.sync.dma_start(out=dst1[:, q, :], in_=sim_sb[:, 128 * q:128 * (q + 1)])
+
+        def t1_next(k):
+            if k < len(seq):
+                t1(k)
+
+        with tc.manual_schedule():
             t1(0)
             t1(1)
-            for i in range(-4, NB):
-                if ok(i):
-                    quant(i)
-                if ok(i + 1):
-                    scale_g(i + 1)
-                    scale_v(i + 1)
-                if ok(i):
-                    mx(i)
-                if ok(i + 2):
-                    bcast_t(i + 2, 1)
-                    rcopy(i + 2)
-                    bcast_t(i + 2, 0)
-                if ok(i + 4):
-                    for s in range(4):
-                        k = 4 * (i + 4) + s
-                        if k + 2 < len(seq):
-                            t1(k + 2)
-                        sumsq(k)
-                        if s == 1:
-                            root(i + 4, 1)
-                    root(i + 4, 0)
-                if ok(i):
-                    reduce(i)
-                if ok(i + 3):
-                    recip(i + 3, 1)
-                    recip(i + 3, 0)
-                if ok(i) and i % 4 == 3 and i < NB - 1:
-                    q = i // 4
-                    fin = mix(q)
-                    nc.scalar.copy(out=sim_sb[:, 128 * q:128 * (q + 1)], in_=fin[:])
-                    nc.sync.dma_start(out=dst1[:, q, :], in_=sim_sb[:, 128 * q:128 * (q + 1)])
-
-        body()
+            for r in range(NB + 3):
+                b = r - 2
+                k = 4 * r
+                if ok(b):
+                    quant(b)
+                t1_next(k + 2)
+                if ok(r):
+                    sumsq(k)
+                if r == 0:
+                    prototypes()
+                if ok(b + 1):
+                    scale_g(b + 1)
+                    recip(b + 1, 0)
+                    bcast_t(b + 1, 0)
+                t1_next(k + 3)
+                if ok(r):
+                    sumsq(k + 1)
+                    root(r, 1)
+                if ok(b - 1):
+                    reduce(b - 1)
+                if ok(b - 1) and (b - 1) % 4 == 3 and b - 1 < NB - 1:
+                    out_sim((b - 1) // 4)
+                if ok(b + 1):
+                    scale_v(b + 1, 1)
+                if ok(r):
+                    recip(r, 1)
+                if ok(b):
+                    mx(b, 1)
+                t1_next(k + 4)
+                if ok(r):
+                    sumsq(k + 2)
+                    bcast_t(r, 1)
+                t1_next(k + 5)
+                if ok(b + 1):
+                    scale_v(b + 1, 0)
+                if ok(r):
+                    sumsq(k + 3)
+                    root(r, 0)
+                    rcopy(r)
+                if ok(b):
+                    mx(b, 0)
 
         nc.scalar.activation(out=mask_sb[:, 0:384], in_=sim_sb[:, 0:384], func=ACT.Sigmoid)
         nc.sync.dma_start(

@@ -16,7 +16,7 @@ AX = mybir.AxisListType
 
 P = 128
 NB = 16
-MVO = 48
+MVO = 112
 
 
 def tile_freedamasker_t_kernel(tc, image_feat, proto_emb, out_0, out_1):

@@ -16,6 +16,7 @@ AX = mybir.AxisListType
 
 P = 128
 NB = 16
+RUN = 4
 MVO = 112
 
 
@@ -56,10 +57,10 @@ def tile_freedamasker_t_kernel(tc, image_feat, proto_emb, out_0, out_1):
         res_max_v = res_max[:].rearrange("p (b n a) -> p b n a", n=4, a=8)
         res_sum_v = res_sum[:].rearrange("p (b n a) -> p b n a", n=4, a=8)
         sim_t = keep.tile([P, 512], F32, name="sim_t")
-        sim_sb = keep.tile([P, 512], F32, name="sim_sb")
-        mask_sb = keep.tile([P, 512], F32, name="mask_sb")
-        dst0 = out_0.rearrange("b n (a r) w -> (b n a) (r w)", a=8).rearrange("(q p) f -> p q f", p=P)
-        dst1 = out_1.rearrange("b n (a r) w -> (b n a) (r w)", a=8).rearrange("(q p) f -> p q f", p=P)
+        sim_sb = keep.tile([P, 2, P, 2], F32, name="sim_sb")
+        mask_sb = keep.tile([P, 2, P, 2], F32, name="mask_sb")
+        dst0 = out_0.rearrange("b n (a r) w -> (b n a) (r w)", a=4).rearrange("(q p) f -> p q f", p=P)
+        dst1 = out_1.rearrange("b n (a r) w -> (b n a) (r w)", a=4).rearrange("(q p) f -> p q f", p=P)
 
         pcodes = keep.tile([P, 384], U32, name="pcodes", align_bytes=64)
         pscl = keep.tile([P, 384], U8, name="pscl", align_bytes=64)
@@ -159,33 +160,32 @@ def tile_freedamasker_t_kernel(tc, image_feat, proto_emb, out_0, out_1):
         def rcopy(b):
             mv = mvo(b)
             if mv < 256:
-                rs = work.tile([P, 256 - mv, 2], F32, name="rs")
-                nc.scalar.copy(out=rs[:], in_=rbs[(b, 1)][:, :, mv:256].rearrange("p e m -> p m e"))
+                rs = work.tile([P, 2, 256 - mv], F32, name="rs")
+                nc.scalar.copy(out=rs[:], in_=rbs[(b, 1)][:, :, mv:256])
                 rss[b] = rs
+
+        def scale(engine, b, h, e, lo, hi, rin):
+            c0 = 512 * h + 256 * e
+            engine.tensor_tensor(
+                out=grps[b][:, 4 * (c0 + lo):4 * (c0 + hi)].rearrange("p (c i t) -> p c t i", i=RUN, t=4),
+                in0=xs[b][:, :, 512 * h + 2 * lo:512 * h + 2 * hi]
+                .rearrange("p t (c i e) -> p e c t i", i=RUN, e=2)[:, e],
+                in1=rin.rearrange("p (c i) -> p c i", i=RUN)
+                .unsqueeze(2).to_broadcast([P, (hi - lo) // RUN, 4, RUN]),
+                op=ALU.mult,
+            )
 
         def scale_g(b):
             mv = mvo(b)
             grp = grpool.tile([P, 4096], BF16, name="grp", align_bytes=64)
             grps[b] = grp
-            if mv < 256:
-                nw = 2 * (256 - mv)
-                nc.gpsimd.tensor_tensor(
-                    out=grp[:, 2048 + 8 * mv:4096].rearrange("p (w t) -> p w t", t=4),
-                    in0=xs[b][:, :, 512 + 2 * mv:1024].rearrange("p t w -> p w t"),
-                    in1=rss[b][:].rearrange("p m e -> p (m e)").unsqueeze(2).to_broadcast([P, nw, 4]),
-                    op=ALU.mult,
-                )
+            for e in range(2):
+                scale(nc.gpsimd, b, 1, e, mv, 256, rss[b][:, e, :])
 
         def scale_v(b, h):
-            grp = grps[b]
             mv = mvo(b) if h else 256
-            nc.vector.tensor_tensor(
-                out=grp[:, 2048 * h:2048 * h + 8 * mv].rearrange("p (m e t) -> p m t e", e=2, t=4),
-                in0=xs[b][:, :, 512 * h:512 * h + 2 * mv].rearrange("p t (m e) -> p m t e", e=2),
-                in1=rbs[(b, h)][:, :, 0:mv].rearrange("p e m -> p m e")
-                .unsqueeze(2).to_broadcast([P, mv, 4, 2]),
-                op=ALU.mult,
-            )
+            for e in range(2):
+                scale(nc.vector, b, h, e, 0, mv, rbs[(b, h)][:, e, 0:mv])
 
         def quant(b):
             codes = work.tile([P, 1024], U32, name="codes", align_bytes=64)
@@ -237,26 +237,31 @@ def tile_freedamasker_t_kernel(tc, image_feat, proto_emb, out_0, out_1):
                 )
 
         def mix(q):
-            cols = slice(128 * q, 128 * (q + 1))
-            tmp = work.tile([P, P], F32, name="tmp")
+            cols = slice(256 * q, 256 * (q + 1))
+            tmp = work.tile([P, 256], F32, name="tmp")
             nc.vector.tensor_scalar(
                 out=tmp[:], in0=res_sum[:, cols], scalar1=1.0 / 64.0, scalar2=None, op0=ALU.mult
             )
-            nc.vector.scalar_tensor_tensor(
-                out=sim_t[:, cols], in0=res_max[:, cols], scalar=0.5, in1=tmp[:],
-                op0=ALU.mult, op1=ALU.add,
-            )
-            fin = ps_xt.tile([P, P], F32, name="xt")
-            nc.tensor.transpose(fin[:], sim_t[:, cols], ident_f[:])
-            return fin
+            fin = ps_xt.tile([P, 2, P], F32, name="xt")
+            for e in range(2):
+                dst = sim_t[:, 256 * q + 128 * e:256 * q + 128 * (e + 1)]
+                nc.vector.scalar_tensor_tensor(
+                    out=dst.rearrange("p (x j) -> p x j", j=2),
+                    in0=res_max[:, cols].rearrange("p (x e j) -> p e x j", e=2, j=2)[:, e],
+                    scalar=0.5,
+                    in1=tmp[:].rearrange("p (x e j) -> p e x j", e=2, j=2)[:, e],
+                    op0=ALU.mult, op1=ALU.add,
+                )
+                nc.tensor.transpose(fin[:, e, :], dst, ident_f[:])
+            return fin[:].rearrange("p e m -> p m e")
 
         def ok(b):
             return 0 <= b < NB
 
         def out_sim(q):
             fin = mix(q)
-            nc.scalar.copy(out=sim_sb[:, 128 * q:128 * (q + 1)], in_=fin[:])
-            nc.sync.dma_start(out=dst1[:, q, :], in_=sim_sb[:, 128 * q:128 * (q + 1)])
+            nc.scalar.copy(out=sim_sb[:, q], in_=fin)
+            nc.sync.dma_start(out=dst1[:, q, :], in_=sim_sb[:, q].rearrange("p m e -> p (m e)"))
 
         def t1_next(k):
             if k < len(seq):
@@ -285,8 +290,8 @@ def tile_freedamasker_t_kernel(tc, image_feat, proto_emb, out_0, out_1):
                     root(r, 1)
                 if ok(b - 1):
                     reduce(b - 1)
-                if ok(b - 1) and (b - 1) % 4 == 3 and b - 1 < NB - 1:
-                    out_sim((b - 1) // 4)
+                if b - 1 == 7:
+                    out_sim(0)
                 if ok(b + 1):
                     scale_v(b + 1, 1)
                 if ok(r):
@@ -307,12 +312,10 @@ def tile_freedamasker_t_kernel(tc, image_feat, proto_emb, out_0, out_1):
                 if ok(b):
                     mx(b, 0)
 
-        nc.scalar.activation(out=mask_sb[:, 0:384], in_=sim_sb[:, 0:384], func=ACT.Sigmoid)
-        nc.sync.dma_start(
-            out=dst0[:, 0:3, :], in_=mask_sb[:, 0:384].rearrange("p (q f) -> p q f", q=3)
-        )
-        fin = mix(3)
-        nc.scalar.activation(out=mask_sb[:, 384:512], in_=fin[:], func=ACT.Sigmoid)
-        nc.vector.tensor_copy(out=sim_sb[:, 384:512], in_=fin[:])
-        nc.sync.dma_start(out=dst0[:, 3, :], in_=mask_sb[:, 384:512])
-        nc.scalar.dma_start(out=dst1[:, 3, :], in_=sim_sb[:, 384:512])
+        nc.scalar.activation(out=mask_sb[:, 0], in_=sim_sb[:, 0], func=ACT.Sigmoid)
+        nc.sync.dma_start(out=dst0[:, 0, :], in_=mask_sb[:, 0].rearrange("p m e -> p (m e)"))
+        fin = mix(1)
+        nc.scalar.activation(out=mask_sb[:, 1], in_=fin, func=ACT.Sigmoid)
+        nc.vector.tensor_copy(out=sim_sb[:, 1], in_=fin)
+        nc.sync.dma_start(out=dst0[:, 1, :], in_=mask_sb[:, 1].rearrange("p m e -> p (m e)"))
+        nc.scalar.dma_start(out=dst1[:, 1, :], in_=sim_sb[:, 1].rearrange("p m e -> p (m e)"))

@@ -16,8 +16,11 @@ AX = mybir.AxisListType
 
 P = 128
 NB = 16
+LAST = NB - 1
+EPS = 1e-12
 RUN = 4
-MVO = 112
+GF = 96
+SF = 384
 
 
 def tile_freedamasker_t_kernel(tc, image_feat, proto_emb, out_0, out_1):
@@ -27,7 +30,7 @@ def tile_freedamasker_t_kernel(tc, image_feat, proto_emb, out_0, out_1):
         small = ctx.enter_context(tc.tile_pool(name="small", bufs=8))
         work = ctx.enter_context(tc.tile_pool(name="work", bufs=2))
         grpool = ctx.enter_context(tc.tile_pool(name="grpool", bufs=1))
-        ps_xt = ctx.enter_context(tc.psum_pool(name="ps_xt", bufs=3))
+        ps_xt = ctx.enter_context(tc.psum_pool(name="ps_xt", bufs=4))
         ps = ctx.enter_context(tc.psum_pool(name="ps", bufs=1))
 
         pro = keep.tile([P, 512], BF16, name="pro")
@@ -37,16 +40,16 @@ def tile_freedamasker_t_kernel(tc, image_feat, proto_emb, out_0, out_1):
             xb = keep.tile([P, 4, 1024], BF16, name="x%d" % b)
             src = image_feat[b].rearrange("(p t) h w -> p t (h w)", t=4)
             if b == 0:
-                for lo, hi in ((512, 768), (768, 1024), (0, 512)):
+                for lo, hi in ((0, 256), (256, 512), (512, 1024)):
                     nc.sync.dma_start(out=xb[:, :, lo:hi], in_=src[:, :, lo:hi])
             else:
                 nc.sync.dma_start(out=xb[:], in_=src)
             xs.append(xb)
 
         eps = keep.tile([P, 1], F32, name="eps")
-        nc.vector.memset(eps[:], 1e-12)
+        nc.vector.memset(eps[:], EPS)
         warm = keep.tile([P, 1], F32, name="warm")
-        nc.scalar.activation(out=warm[:], in_=eps[:], func=ACT.Sqrt)
+        nc.scalar.activation(out=warm[:], in_=eps[:], func=ACT.Abs_reciprocal_sqrt)
         ident_f = keep.tile([P, P], F32, name="ident_f")
         make_identity(nc, ident_f[:])
         ident_b = keep.tile([P, P], BF16, name="ident_b")
@@ -56,7 +59,8 @@ def tile_freedamasker_t_kernel(tc, image_feat, proto_emb, out_0, out_1):
         res_sum = keep.tile([P, 512], F32, name="res_sum")
         res_max_v = res_max[:].rearrange("p (b n a) -> p b n a", n=4, a=8)
         res_sum_v = res_sum[:].rearrange("p (b n a) -> p b n a", n=4, a=8)
-        sim_t = keep.tile([P, 512], F32, name="sim_t")
+        half_mean = keep.tile([P, 512], F32, name="half_mean")
+        sim_t = keep.tile([P, 2, 2, P], F32, name="sim_t")
         sim_sb = keep.tile([P, 2, P, 2], F32, name="sim_sb")
         mask_sb = keep.tile([P, 2, P, 2], F32, name="mask_sb")
         dst0 = out_0.rearrange("b n (a r) w -> (b n a) (r w)", a=4).rearrange("(q p) f -> p q f", p=P)
@@ -72,16 +76,16 @@ def tile_freedamasker_t_kernel(tc, image_feat, proto_emb, out_0, out_1):
                 out=psq[:], in0=pro[:], scalar=1.0, in1=pro[:],
                 op0=ALU.mult, op1=ALU.mult, accum_out=pss[:],
             )
-            pnrm = keep.tile([P, 1], F32, name="pnrm")
-            nc.scalar.activation(out=pnrm[:], in_=pss[:], func=ACT.Sqrt, bias=eps[:, 0:1])
             prin = keep.tile([P, 1], F32, name="prin")
-            nc.vector.reciprocal(out=prin[:], in_=pnrm[:])
+            nc.scalar.activation(
+                out=prin[:], in_=pss[:], func=ACT.Abs_reciprocal_sqrt, bias=eps[:, 0:1]
+            )
             pn = keep.tile([P, 4, P], BF16, name="pn")
             nc.vector.tensor_scalar(
                 out=pn[:], in0=pro[:].rearrange("m (p t) -> m t p", t=4),
                 scalar1=prin[:, 0:1], scalar2=None, op0=ALU.mult,
             )
-            pt_ps = ps.tile([P, 4, P], BF16, name="pt_ps", tag="o0")
+            pt_ps = ps.tile([P, 4, P], BF16, name="pt_ps", tag="o")
             for t in range(4):
                 nc.tensor.transpose(pt_ps[:, t, :], pn[:, t, :], ident_b[:])
             pgrp = keep.tile([P, 384, 4], BF16, name="pgrp", align_bytes=64)
@@ -97,10 +101,8 @@ def tile_freedamasker_t_kernel(tc, image_feat, proto_emb, out_0, out_1):
                     in_=pgrp[:, lo:hi, :].rearrange("p m t -> p (m t)"),
                 )
 
-
         xts = {}
         sss = {}
-        nrms = {}
         rins = {}
         rbs = {}
         rss = {}
@@ -108,13 +110,13 @@ def tile_freedamasker_t_kernel(tc, image_feat, proto_emb, out_0, out_1):
         cds = {}
         outs = {}
         sums = {}
-        seq = [(b, u) for b in range(NB) for u in (2, 3, 0, 1)]
-
-        def mvo(b):
-            return 160 if b == 0 else MVO
+        xns = {}
+        bks = {}
 
         def t1(k):
-            b, u = seq[k]
+            if k >= 4 * NB:
+                return
+            b, u = divmod(k, 4)
             xw = xs[b][:].bitcast(F32)
             xt = ps_xt.tile([P, 512], F32, name="xt")
             for t in range(4):
@@ -123,28 +125,23 @@ def tile_freedamasker_t_kernel(tc, image_feat, proto_emb, out_0, out_1):
                 )
             xts[k] = xt
 
-        def sumsq(k):
-            b, u = seq[k]
+        def sumsq(k, e):
+            b, u = divmod(k, 4)
             h, j = divmod(u, 2)
-            if j == 0:
+            if j == 0 and e == 0:
                 sss[(b, h)] = small.tile([P, 4], F32, name="ss")
             v = xts[k][:].bitcast(BF16).rearrange("p (c e) -> p c e", e=2)
-            for e in range(2):
-                junk = work.tile([P, 512], BF16, name="junk")
-                nc.scalar.activation(
-                    out=junk[:], in_=v[:, :, e], func=ACT.Square,
-                    accum_out=sss[(b, h)][:, 2 * j + e:2 * j + e + 1],
-                )
+            junk = work.tile([P, 512], BF16, name="junk")
+            nc.scalar.activation(
+                out=junk[:], in_=v[:, :, e], func=ACT.Square,
+                accum_out=sss[(b, h)][:, 2 * j + e:2 * j + e + 1],
+            )
 
         def root(b, h):
-            nrm = small.tile([P, 4], F32, name="nrm")
-            nc.scalar.activation(out=nrm[:], in_=sss[(b, h)][:], func=ACT.Sqrt, bias=eps[:, 0:1])
-            nrms[(b, h)] = nrm
-
-        def recip(b, h):
-            rin = small.tile([P, 4], F32, name="rin")
-            nc.vector.reciprocal(out=rin[:], in_=nrms[(b, h)][:])
-            rins[(b, h)] = rin
+            rins[(b, h)] = small.tile([P, 4], F32, name="rin")
+            nc.scalar.activation(
+                out=rins[(b, h)][:], in_=sss[(b, h)][:], func=ACT.Abs_reciprocal_sqrt, bias=eps[:, 0:1]
+            )
 
         def bcast_t(b, h):
             rp = ps.tile([P, 2, 256], F32, name="rp", tag="rp%d" % h)
@@ -158,11 +155,9 @@ def tile_freedamasker_t_kernel(tc, image_feat, proto_emb, out_0, out_1):
             rbs[(b, h)] = rp
 
         def rcopy(b):
-            mv = mvo(b)
-            if mv < 256:
-                rs = work.tile([P, 2, 256 - mv], F32, name="rs")
-                nc.scalar.copy(out=rs[:], in_=rbs[(b, 1)][:, :, mv:256])
-                rss[b] = rs
+            rs = work.tile([P, SF - GF], F32, name="rs")
+            nc.scalar.copy(out=rs[:], in_=rbs[(b, 0)][:].rearrange("p e m -> p (e m)")[:, GF:SF])
+            rss[b] = rs
 
         def scale(engine, b, h, e, lo, hi, rin):
             c0 = 512 * h + 256 * e
@@ -176,146 +171,184 @@ def tile_freedamasker_t_kernel(tc, image_feat, proto_emb, out_0, out_1):
             )
 
         def scale_g(b):
-            mv = mvo(b)
-            grp = grpool.tile([P, 4096], BF16, name="grp", align_bytes=64)
-            grps[b] = grp
-            for e in range(2):
-                scale(nc.gpsimd, b, 1, e, mv, 256, rss[b][:, e, :])
+            grps[b] = grpool.tile([P, 4096], BF16, name="grp", align_bytes=64)
+            scale(nc.gpsimd, b, 0, 0, GF, 256, rss[b][:, 0:256 - GF])
+            scale(nc.gpsimd, b, 0, 1, 0, SF - 256, rss[b][:, 256 - GF:SF - GF])
 
-        def scale_v(b, h):
-            mv = mvo(b) if h else 256
-            for e in range(2):
-                scale(nc.vector, b, h, e, 0, mv, rbs[(b, h)][:, e, 0:mv])
+        def scale_v(b, h, e, lo, hi):
+            scale(nc.vector, b, h, e, lo, hi, rbs[(b, h)][:, e, lo:hi])
 
-        def quant(b):
-            codes = work.tile([P, 1024], U32, name="codes", align_bytes=64)
-            scl = work.tile([P, 1024], U8, name="scl", align_bytes=64)
-            nc.vector.quantize_mx(out=codes[:].bitcast(FP8X4), scales=scl[:], in_=grps[b][:])
-            cds[b] = (codes, scl)
-
-        def mx(b, hh):
-            codes, scl = cds[b]
-            for h in (hh,):
-                o = ps.tile([P, 512], F32, name="o", tag="o%d" % h)
-                for j in range(4):
-                    cols = slice(512 * h + 128 * j, 512 * h + 128 * (j + 1))
-                    nc.tensor.matmul_mx(
-                        out=o[:, 128 * j:128 * (j + 1)],
-                        lhsT=codes[:, cols].bitcast(FP8X4), lhsT_scale=scl[:, cols],
-                        rhs=pcodes[:, 256:384].bitcast(FP8X4), rhs_scale=pscl[:, 256:384],
-                        start=True, stop=True,
-                    )
-                outs[(b, h)] = o
-            if hh == 1:
-                sums[b] = ps.tile([P, 512], F32, name="sm", tag="sm")
-            sm = sums[b]
-            for j in range(4 * (1 - hh), 4 * (1 - hh) + 4):
-                c0 = 128 * ((j + 4) % 8)
-                cols = slice(c0, c0 + 128)
-                for s in range(4):
-                    pc = slice(64 * s, 64 * s + 128)
-                    nc.tensor.matmul_mx(
-                        out=sm[:, 32 * j:32 * j + 128],
-                        lhsT=codes[:, cols].bitcast(FP8X4), lhsT_scale=scl[:, cols],
-                        rhs=pcodes[:, pc].bitcast(FP8X4), rhs_scale=pscl[:, pc],
-                        start=(s == 0), stop=(s == 3),
-                    )
-
-        def reduce(b):
-            for h in (1, 0):
-                ov = outs[(b, h)][:].rearrange("p (j n k) -> p j n k", n=4, k=32)
-                a0 = 4 * h
-                nc.vector.tensor_reduce(
-                    out=res_max_v[:, b, :, a0:a0 + 4].rearrange("p n j -> p j n"),
-                    in_=ov, axis=AX.X, op=ALU.max,
-                )
-            for h in (1, 0):
-                nc.vector.tensor_reduce(
-                    out=res_sum_v[:, b, :, 4 * h:4 * h + 4].rearrange("p n j -> p j n"),
-                    in_=sums[b][:, 128 * (1 - h):128 * (2 - h)].rearrange("p (j n g) -> p j n g", n=4, g=8),
-                    axis=AX.X, op=ALU.add,
-                )
-
-        def mix(q):
-            cols = slice(256 * q, 256 * (q + 1))
-            tmp = work.tile([P, 256], F32, name="tmp")
-            nc.vector.tensor_scalar(
-                out=tmp[:], in0=res_sum[:, cols], scalar1=1.0 / 64.0, scalar2=None, op0=ALU.mult
+        def scale_s(b):
+            xn = work.tile([P, 512], BF16, name="xn")
+            v = xts[4 * b + 1][:].bitcast(BF16).rearrange("m (u f p e) -> m e u p f", u=2, f=2, e=2)
+            nc.scalar.activation(
+                out=xn[:].rearrange("m (u p f) -> m u p f", u=2, f=2), in_=v[:, 1],
+                func=ACT.Copy, scale=rins[(b, 0)][:, 3:4],
             )
-            fin = ps_xt.tile([P, 2, P], F32, name="xt")
+            xns[b] = xn
+
+        def back_t(b):
+            bk = ps_xt.tile([P, 2, P], F32, name="xt")
+            words = xns[b][:].bitcast(F32)
+            for u in range(2):
+                nc.tensor.transpose(bk[:, u, :], words[:, 128 * u:128 * (u + 1)], ident_f[:])
+            bks[b] = bk
+
+        def back_copy(b):
+            nc.scalar.copy(
+                out=grps[b][:, 4 * SF:2048].bitcast(F32).rearrange("p (m u) -> p m u", u=2),
+                in_=bks[b][:].rearrange("p u m -> p m u"),
+            )
+
+        def quant(b, h0, h1):
+            if h0 == 0:
+                codes = work.tile([P, 1024], U32, name="codes", align_bytes=64)
+                scl = work.tile([P, 1024], U8, name="scl", align_bytes=64)
+                cds[b] = (codes, scl)
+            codes, scl = cds[b]
+            cols = slice(512 * h0, 512 * h1)
+            nc.vector.quantize_mx(
+                out=codes[:, cols].bitcast(FP8X4), scales=scl[:, cols],
+                in_=grps[b][:, 2048 * h0:2048 * h1],
+            )
+
+        def mx(b, h, out, col, pcol, start, stop):
+            codes, scl = cds[b]
+            nc.tensor.matmul_mx(
+                out=out[:, col:col + 128],
+                lhsT=codes[:, h:h + 128].bitcast(FP8X4), lhsT_scale=scl[:, h:h + 128],
+                rhs=pcodes[:, pcol:pcol + 128].bitcast(FP8X4), rhs_scale=pscl[:, pcol:pcol + 128],
+                start=start, stop=stop,
+            )
+
+        def mx_all(b, h, tag):
+            o = ps.tile([P, 512], F32, name="o", tag=tag)
+            for j in range(4):
+                mx(b, 512 * h + 128 * j, o, 128 * j, 256, True, True)
+            outs[(b, h)] = o
+
+        def mx_sum(b, h):
+            if h == 0:
+                sums[b] = ps.tile([P, 512], F32, name="sm")
+            for j in range(4 * h, 4 * h + 4):
+                for s in range(4):
+                    mx(b, 128 * j, sums[b], 32 * j, 64 * s, s == 0, s == 3)
+
+        def top(b, h):
+            nc.vector.tensor_reduce(
+                out=res_max_v[:, b, :, 4 * h:4 * h + 4].rearrange("p n j -> p j n"),
+                in_=outs[(b, h)][:].rearrange("p (j n k) -> p j n k", n=4, k=32),
+                axis=AX.X, op=ALU.max,
+            )
+
+        def add(b):
+            nc.vector.tensor_reduce(
+                out=res_sum_v[:, b].rearrange("p n j -> p j n"),
+                in_=sums[b][:, 0:256].rearrange("p (j n g) -> p j n g", n=4, g=8),
+                axis=AX.X, op=ALU.add,
+            )
+
+        def mean(lo, hi):
+            cols = slice(32 * lo, 32 * hi)
+            nc.vector.tensor_scalar(
+                out=half_mean[:, cols], in0=res_sum[:, cols], scalar1=1.0 / 64.0, scalar2=None, op0=ALU.mult
+            )
+
+        def mix(lo, hi):
+            cols = slice(32 * lo, 32 * hi)
+            q, x = divmod(lo, 8)
             for e in range(2):
-                dst = sim_t[:, 256 * q + 128 * e:256 * q + 128 * (e + 1)]
                 nc.vector.scalar_tensor_tensor(
-                    out=dst.rearrange("p (x j) -> p x j", j=2),
+                    out=sim_t[:, q, e, 16 * x:16 * (x + hi - lo)].rearrange("p (x j) -> p x j", j=2),
                     in0=res_max[:, cols].rearrange("p (x e j) -> p e x j", e=2, j=2)[:, e],
                     scalar=0.5,
-                    in1=tmp[:].rearrange("p (x e j) -> p e x j", e=2, j=2)[:, e],
+                    in1=half_mean[:, cols].rearrange("p (x e j) -> p e x j", e=2, j=2)[:, e],
                     op0=ALU.mult, op1=ALU.add,
                 )
-                nc.tensor.transpose(fin[:, e, :], dst, ident_f[:])
+
+        def fin_t(q):
+            fin = ps_xt.tile([P, 2, P], F32, name="xt")
+            for e in range(2):
+                nc.tensor.transpose(fin[:, e, :], sim_t[:, q, e, :], ident_f[:])
             return fin[:].rearrange("p e m -> p m e")
 
         def ok(b):
             return 0 <= b < NB
 
-        def out_sim(q):
-            fin = mix(q)
-            nc.scalar.copy(out=sim_sb[:, q], in_=fin)
-            nc.sync.dma_start(out=dst1[:, q, :], in_=sim_sb[:, q].rearrange("p m e -> p (m e)"))
-
-        def t1_next(k):
-            if k < len(seq):
-                t1(k)
-
         with tc.manual_schedule():
             t1(0)
             t1(1)
-            for r in range(NB + 3):
-                b = r - 2
+            prototypes()
+            for r in range(NB + 1):
                 k = 4 * r
-                if ok(b):
-                    quant(b)
-                t1_next(k + 2)
+                t1(k + 2)
                 if ok(r):
-                    sumsq(k)
-                if r == 0:
-                    prototypes()
-                if ok(b + 1):
-                    scale_g(b + 1)
-                    recip(b + 1, 0)
-                    bcast_t(b + 1, 0)
-                t1_next(k + 3)
+                    sumsq(k, 0)
+                if ok(r - 1):
+                    root(r - 1, 1)
+                    bcast_t(r - 1, 1)
+                    back_copy(r - 1)
+                t1(k + 3)
                 if ok(r):
-                    sumsq(k + 1)
-                    root(r, 1)
-                if ok(b - 1):
-                    reduce(b - 1)
-                if b - 1 == 7:
-                    out_sim(0)
-                if ok(b + 1):
-                    scale_v(b + 1, 1)
+                    sumsq(k, 1)
+                if ok(r - 2):
+                    mx_all(r - 2, 0, "o")
+                    mx_sum(r - 2, 0)
+                if ok(r - 1):
+                    scale_v(r - 1, 1, 0, 0, 256)
+                if ok(r - 2):
+                    top(r - 2, 0)
+                if ok(r - 1):
+                    scale_v(r - 1, 1, 1, 0, 256)
+                    quant(r - 1, 0, 2)
                 if ok(r):
-                    recip(r, 1)
-                if ok(b):
-                    mx(b, 1)
-                t1_next(k + 4)
-                if ok(r):
-                    sumsq(k + 2)
-                    bcast_t(r, 1)
-                t1_next(k + 5)
-                if ok(b + 1):
-                    scale_v(b + 1, 0)
-                if ok(r):
-                    sumsq(k + 3)
+                    sumsq(k + 1, 0)
+                    sumsq(k + 1, 1)
+                    sumsq(k + 2, 0)
                     root(r, 0)
+                    bcast_t(r, 0)
+                if ok(r - 2):
+                    mx_all(r - 2, 1, "o")
+                    top(r - 2, 1)
+                if ok(r):
+                    sumsq(k + 2, 1)
+                    scale_s(r)
+                    back_t(r)
+                t1(k + 4)
+                t1(k + 5)
+                if ok(r - 2):
+                    mx_sum(r - 2, 1)
+                if ok(r):
+                    sumsq(k + 3, 0)
                     rcopy(r)
-                if ok(b):
-                    mx(b, 0)
+                    scale_g(r)
+                    scale_v(r, 0, 0, 0, GF)
+                    sumsq(k + 3, 1)
+                if ok(r - 2):
+                    add(r - 2)
+                    if r - 2 == 7:
+                        mean(0, 8)
+                    if r - 2 == 8:
+                        mix(0, 8)
 
-        nc.scalar.activation(out=mask_sb[:, 0], in_=sim_sb[:, 0], func=ACT.Sigmoid)
-        nc.sync.dma_start(out=dst0[:, 0, :], in_=mask_sb[:, 0].rearrange("p m e -> p (m e)"))
-        fin = mix(1)
-        nc.scalar.activation(out=mask_sb[:, 1], in_=fin, func=ACT.Sigmoid)
-        nc.vector.tensor_copy(out=sim_sb[:, 1], in_=fin)
-        nc.sync.dma_start(out=dst0[:, 1, :], in_=mask_sb[:, 1].rearrange("p m e -> p (m e)"))
-        nc.scalar.dma_start(out=dst1[:, 1, :], in_=sim_sb[:, 1].rearrange("p m e -> p (m e)"))
+            fin = fin_t(0)
+            nc.scalar.activation(out=mask_sb[:, 0], in_=fin, func=ACT.Sigmoid)
+            nc.scalar.copy(out=sim_sb[:, 0], in_=fin)
+            nc.sync.dma_start(out=dst0[:, 0, :], in_=mask_sb[:, 0].rearrange("p m e -> p (m e)"))
+            nc.sync.dma_start(out=dst1[:, 0, :], in_=sim_sb[:, 0].rearrange("p m e -> p (m e)"))
+            mx_all(LAST, 0, "o")
+            mx_all(LAST, 1, "rp0")
+            mx_sum(LAST, 0)
+            mx_sum(LAST, 1)
+            mean(8, LAST)
+            top(LAST, 0)
+            mix(8, LAST)
+            top(LAST, 1)
+            add(LAST)
+            mean(LAST, NB)
+            mix(LAST, NB)
+            fin = fin_t(1)
+            nc.scalar.activation(out=mask_sb[:, 1], in_=fin, func=ACT.Sigmoid)
+            nc.vector.tensor_copy(out=sim_sb[:, 1], in_=fin)
+            nc.sync.dma_start(out=dst0[:, 1, :], in_=mask_sb[:, 1].rearrange("p m e -> p (m e)"))
+            nc.scalar.dma_start(out=dst1[:, 1, :], in_=sim_sb[:, 1].rearrange("p m e -> p (m e)"))

@@ -21,6 +21,8 @@ EPS = 1e-12
 RUN = 4
 GF = 96
 SF = 384
+S_SKIP = (0, 1, 2)
+GF_LAST = 256
 
 
 def tile_freedamasker_t_kernel(tc, image_feat, proto_emb, out_0, out_1):
@@ -60,6 +62,7 @@ def tile_freedamasker_t_kernel(tc, image_feat, proto_emb, out_0, out_1):
         res_max_v = res_max[:].rearrange("p (b n a) -> p b n a", n=4, a=8)
         res_sum_v = res_sum[:].rearrange("p (b n a) -> p b n a", n=4, a=8)
         half_mean = keep.tile([P, 512], F32, name="half_mean")
+        half_max = keep.tile([P, 512], F32, name="half_max")
         sim_t = keep.tile([P, 2, 2, P], F32, name="sim_t")
         sim_sb = keep.tile([P, 2, P, 2], F32, name="sim_sb")
         mask_sb = keep.tile([P, 2, P, 2], F32, name="mask_sb")
@@ -113,6 +116,9 @@ def tile_freedamasker_t_kernel(tc, image_feat, proto_emb, out_0, out_1):
         xns = {}
         bks = {}
 
+        def gf(b):
+            return GF_LAST if b == LAST else GF
+
         def t1(k):
             if k >= 4 * NB:
                 return
@@ -143,10 +149,10 @@ def tile_freedamasker_t_kernel(tc, image_feat, proto_emb, out_0, out_1):
                 out=rins[(b, h)][:], in_=sss[(b, h)][:], func=ACT.Abs_reciprocal_sqrt, bias=eps[:, 0:1]
             )
 
-        def bcast_t(b, h):
+        def bcast_t(b, h, parities=(0, 1)):
             rp = ps.tile([P, 2, 256], F32, name="rp", tag="rp%d" % h)
             for j in range(2):
-                for e in range(2):
+                for e in parities:
                     c = 2 * j + e
                     nc.tensor.transpose(
                         rp[:, e, 128 * j:128 * (j + 1)],
@@ -155,8 +161,9 @@ def tile_freedamasker_t_kernel(tc, image_feat, proto_emb, out_0, out_1):
             rbs[(b, h)] = rp
 
         def rcopy(b):
-            rs = work.tile([P, SF - GF], F32, name="rs")
-            nc.scalar.copy(out=rs[:], in_=rbs[(b, 0)][:].rearrange("p e m -> p (e m)")[:, GF:SF])
+            lo = gf(b)
+            rs = work.tile([P, SF - lo], F32, name="rs")
+            nc.scalar.copy(out=rs[:], in_=rbs[(b, 0)][:].rearrange("p e m -> p (e m)")[:, lo:SF])
             rss[b] = rs
 
         def scale(engine, b, h, e, lo, hi, rin):
@@ -172,33 +179,35 @@ def tile_freedamasker_t_kernel(tc, image_feat, proto_emb, out_0, out_1):
 
         def scale_g(b):
             grps[b] = grpool.tile([P, 4096], BF16, name="grp", align_bytes=64)
-            scale(nc.gpsimd, b, 0, 0, GF, 256, rss[b][:, 0:256 - GF])
-            scale(nc.gpsimd, b, 0, 1, 0, SF - 256, rss[b][:, 256 - GF:SF - GF])
+            lo = gf(b)
+            if lo < 256:
+                scale(nc.gpsimd, b, 0, 0, lo, 256, rss[b][:, 0:256 - lo])
+            scale(nc.gpsimd, b, 0, 1, 0, SF - 256, rss[b][:, 256 - lo:SF - lo])
 
         def scale_v(b, h, e, lo, hi):
             scale(nc.vector, b, h, e, lo, hi, rbs[(b, h)][:, e, lo:hi])
 
-        def scale_s(b):
+        def scale_s(b, h, j, e):
             xn = work.tile([P, 512], BF16, name="xn")
-            v = xts[4 * b + 1][:].bitcast(BF16).rearrange("m (u f p e) -> m e u p f", u=2, f=2, e=2)
+            v = xts[4 * b + 2 * h + j][:].bitcast(BF16).rearrange("m (u f p e) -> m e u p f", u=2, f=2, e=2)
             nc.scalar.activation(
-                out=xn[:].rearrange("m (u p f) -> m u p f", u=2, f=2), in_=v[:, 1],
-                func=ACT.Copy, scale=rins[(b, 0)][:, 3:4],
+                out=xn[:].rearrange("m (u p f) -> m u p f", u=2, f=2), in_=v[:, e],
+                func=ACT.Copy, scale=rins[(b, h)][:, 2 * j + e:2 * j + e + 1],
             )
-            xns[b] = xn
+            xns[(b, h, j, e)] = xn
 
-        def back_t(b):
+        def back_t(b, h, j, e):
             bk = ps_xt.tile([P, 2, P], F32, name="xt")
-            words = xns[b][:].bitcast(F32)
+            words = xns[(b, h, j, e)][:].bitcast(F32)
             for u in range(2):
                 nc.tensor.transpose(bk[:, u, :], words[:, 128 * u:128 * (u + 1)], ident_f[:])
-            bks[b] = bk
+            bks[(b, h, j, e)] = bk
 
-        def back_copy(b):
-            nc.scalar.copy(
-                out=grps[b][:, 4 * SF:2048].bitcast(F32).rearrange("p (m u) -> p m u", u=2),
-                in_=bks[b][:].rearrange("p u m -> p m u"),
-            )
+        def back_copy(b, h, j, e):
+            c0 = 512 * h + 256 * e + 128 * j
+            out = grps[b][:, 4 * c0:4 * (c0 + 128)].bitcast(F32).rearrange("p (m u) -> p m u", u=2)
+            in_ = bks[(b, h, j, e)][:].rearrange("p u m -> p m u")
+            nc.scalar.copy(out=out, in_=in_)
 
         def quant(b, h0, h1):
             if h0 == 0:
@@ -241,29 +250,27 @@ def tile_freedamasker_t_kernel(tc, image_feat, proto_emb, out_0, out_1):
                 axis=AX.X, op=ALU.max,
             )
 
-        def add(b):
+        def add(b, j0=0):
             nc.vector.tensor_reduce(
-                out=res_sum_v[:, b].rearrange("p n j -> p j n"),
-                in_=sums[b][:, 0:256].rearrange("p (j n g) -> p j n g", n=4, g=8),
+                out=res_sum_v[:, b, :, j0:8].rearrange("p n j -> p j n"),
+                in_=sums[b][:, 32 * j0:256].rearrange("p (j n g) -> p j n g", n=4, g=8),
                 axis=AX.X, op=ALU.add,
             )
 
-        def mean(lo, hi):
-            cols = slice(32 * lo, 32 * hi)
-            nc.vector.tensor_scalar(
-                out=half_mean[:, cols], in0=res_sum[:, cols], scalar1=1.0 / 64.0, scalar2=None, op0=ALU.mult
-            )
-
-        def mix(lo, hi):
+        def mix(engine, lo, hi):
             cols = slice(32 * lo, 32 * hi)
             q, x = divmod(lo, 8)
+            for dst, src, factor in ((half_mean, res_sum, 1.0 / 64.0), (half_max, res_max, 0.5)):
+                engine.tensor_scalar(
+                    out=dst[:, cols], in0=src[:, cols],
+                    scalar1=factor, scalar2=0.0, op0=ALU.mult, op1=ALU.add,
+                )
             for e in range(2):
-                nc.vector.scalar_tensor_tensor(
+                engine.tensor_tensor(
                     out=sim_t[:, q, e, 16 * x:16 * (x + hi - lo)].rearrange("p (x j) -> p x j", j=2),
-                    in0=res_max[:, cols].rearrange("p (x e j) -> p e x j", e=2, j=2)[:, e],
-                    scalar=0.5,
+                    in0=half_max[:, cols].rearrange("p (x e j) -> p e x j", e=2, j=2)[:, e],
                     in1=half_mean[:, cols].rearrange("p (x e j) -> p e x j", e=2, j=2)[:, e],
-                    op0=ALU.mult, op1=ALU.add,
+                    op=ALU.add,
                 )
 
         def fin_t(q):
@@ -279,7 +286,7 @@ def tile_freedamasker_t_kernel(tc, image_feat, proto_emb, out_0, out_1):
             t1(0)
             t1(1)
             prototypes()
-            for r in range(NB + 1):
+            for r in range(NB):
                 k = 4 * r
                 t1(k + 2)
                 if ok(r):
@@ -287,7 +294,8 @@ def tile_freedamasker_t_kernel(tc, image_feat, proto_emb, out_0, out_1):
                 if ok(r - 1):
                     root(r - 1, 1)
                     bcast_t(r - 1, 1)
-                    back_copy(r - 1)
+                    if r - 1 not in S_SKIP:
+                        back_copy(r - 1, 0, 1, 1)
                 t1(k + 3)
                 if ok(r):
                     sumsq(k, 1)
@@ -300,10 +308,11 @@ def tile_freedamasker_t_kernel(tc, image_feat, proto_emb, out_0, out_1):
                     top(r - 2, 0)
                 if ok(r - 1):
                     scale_v(r - 1, 1, 1, 0, 256)
-                    quant(r - 1, 0, 2)
+                    quant(r - 1, 0, 1)
+                    quant(r - 1, 1, 2)
                 if ok(r):
-                    sumsq(k + 1, 0)
-                    sumsq(k + 1, 1)
+                    for e in range(2):
+                        sumsq(k + 1, e)
                     sumsq(k + 2, 0)
                     root(r, 0)
                     bcast_t(r, 0)
@@ -312,8 +321,9 @@ def tile_freedamasker_t_kernel(tc, image_feat, proto_emb, out_0, out_1):
                     top(r - 2, 1)
                 if ok(r):
                     sumsq(k + 2, 1)
-                    scale_s(r)
-                    back_t(r)
+                    if r not in S_SKIP:
+                        scale_s(r, 0, 1, 1)
+                        back_t(r, 0, 1, 1)
                 t1(k + 4)
                 t1(k + 5)
                 if ok(r - 2):
@@ -322,31 +332,53 @@ def tile_freedamasker_t_kernel(tc, image_feat, proto_emb, out_0, out_1):
                     sumsq(k + 3, 0)
                     rcopy(r)
                     scale_g(r)
-                    scale_v(r, 0, 0, 0, GF)
+                    scale_v(r, 0, 0, 0, gf(r))
+                    if r in S_SKIP:
+                        scale_v(r, 0, 1, SF - 256, 256)
                     sumsq(k + 3, 1)
                 if ok(r - 2):
                     add(r - 2)
                     if r - 2 == 7:
-                        mean(0, 8)
-                    if r - 2 == 8:
-                        mix(0, 8)
+                        mix(nc.gpsimd, 0, 8)
+                    if r - 2 == 13:
+                        mix(nc.gpsimd, 8, 14)
 
+            root(LAST, 1)
+            bcast_t(LAST, 1, (0,))
+            back_copy(LAST, 0, 1, 1)
+            mx_all(LAST - 1, 0, "o")
+            scale_v(LAST, 1, 0, 0, 256)
+            for j in range(2):
+                scale_s(LAST, 1, j, 1)
+                back_t(LAST, 1, j, 1)
+            mx_sum(LAST - 1, 0)
+            top(LAST - 1, 0)
+            for j in range(2):
+                back_copy(LAST, 1, j, 1)
+            mx_all(LAST - 1, 1, "o")
+            mx_sum(LAST - 1, 1)
+            quant(LAST, 0, 1)
+            top(LAST - 1, 1)
+            quant(LAST, 1, 2)
             fin = fin_t(0)
             nc.scalar.activation(out=mask_sb[:, 0], in_=fin, func=ACT.Sigmoid)
             nc.scalar.copy(out=sim_sb[:, 0], in_=fin)
             nc.sync.dma_start(out=dst0[:, 0, :], in_=mask_sb[:, 0].rearrange("p m e -> p (m e)"))
             nc.sync.dma_start(out=dst1[:, 0, :], in_=sim_sb[:, 0].rearrange("p m e -> p (m e)"))
-            mx_all(LAST, 0, "o")
-            mx_all(LAST, 1, "rp0")
-            mx_sum(LAST, 0)
+            add(LAST - 1)
+            mx_all(LAST, 0, "rp0")
+            mx_all(LAST, 1, "rp1")
+            sums[LAST] = ps.tile([P, 512], F32, name="sm")
             mx_sum(LAST, 1)
-            mean(8, LAST)
             top(LAST, 0)
-            mix(8, LAST)
+            nc.vector.tensor_reduce(
+                out=res_sum_v[:, LAST, :, 0:4].rearrange("p n j -> p j n"),
+                in_=outs[(LAST, 0)][:].rearrange("p (j n k) -> p j n k", n=4, k=32),
+                axis=AX.X, op=ALU.add,
+            )
             top(LAST, 1)
-            add(LAST)
-            mean(LAST, NB)
-            mix(LAST, NB)
+            add(LAST, 4)
+            mix(nc.vector, 14, NB)
             fin = fin_t(1)
             nc.scalar.activation(out=mask_sb[:, 1], in_=fin, func=ACT.Sigmoid)
             nc.vector.tensor_copy(out=sim_sb[:, 1], in_=fin)

@@ -21,8 +21,8 @@ EPS = 1e-12
 RUN = 4
 GF = 96
 SF = 384
-S_SKIP = (0, 1, 2)
-GF_LAST = 256
+S_SKIP = tuple(b for b in range(NB) if b == 0 or b == 1 or (b % 3 == 2 and b < LAST - 1))
+GF_LAST = 160
 
 
 def tile_freedamasker_t_kernel(tc, image_feat, proto_emb, out_0, out_1):
@@ -149,11 +149,13 @@ def tile_freedamasker_t_kernel(tc, image_feat, proto_emb, out_0, out_1):
                 out=rins[(b, h)][:], in_=sss[(b, h)][:], func=ACT.Abs_reciprocal_sqrt, bias=eps[:, 0:1]
             )
 
-        def bcast_t(b, h, parities=(0, 1)):
+        def bcast_t(b, h, skip=()):
             rp = ps.tile([P, 2, 256], F32, name="rp", tag="rp%d" % h)
             for j in range(2):
-                for e in parities:
+                for e in range(2):
                     c = 2 * j + e
+                    if c in skip:
+                        continue
                     nc.tensor.transpose(
                         rp[:, e, 128 * j:128 * (j + 1)],
                         rins[(b, h)][:, c:c + 1].to_broadcast([P, P]), ident_f[:],
@@ -315,7 +317,7 @@ def tile_freedamasker_t_kernel(tc, image_feat, proto_emb, out_0, out_1):
                         sumsq(k + 1, e)
                     sumsq(k + 2, 0)
                     root(r, 0)
-                    bcast_t(r, 0)
+                    bcast_t(r, 0, () if r in S_SKIP else (3,))
                 if ok(r - 2):
                     mx_all(r - 2, 1, "o")
                     top(r - 2, 1)
@@ -344,7 +346,7 @@ def tile_freedamasker_t_kernel(tc, image_feat, proto_emb, out_0, out_1):
                         mix(nc.gpsimd, 8, 14)
 
             root(LAST, 1)
-            bcast_t(LAST, 1, (0,))
+            bcast_t(LAST, 1, (1, 3))
             back_copy(LAST, 0, 1, 1)
             mx_all(LAST - 1, 0, "o")
             scale_v(LAST, 1, 0, 0, 256)

from contextlib import ExitStack

import concourse.mybir as mybir
from concourse.masks import make_identity

FLOPS = 2 * 16384 * 512 * 128

BF16 = mybir.dt.bfloat16
F32 = mybir.dt.float32
U32 = mybir.dt.uint32
U8 = mybir.dt.uint8
FP8X4 = mybir.dt.float8_e4m3fn_x4
ACT = mybir.ActivationFunctionType
ALU = mybir.AluOpType
AX = mybir.AxisListType

P = 128
NB = 16
LAST = NB - 1
EPS = 1e-12
RUN = 4
GF = 96
SF = 384
S_SKIP = tuple(b for b in range(NB) if b == 0 or b == 1 or (b % 3 == 2 and b < LAST - 1))
GF_LAST = 160


def tile_freedamasker_t_kernel(tc, image_feat, proto_emb, out_0, out_1):
    nc = tc.nc
    with ExitStack() as ctx:
        keep = ctx.enter_context(tc.tile_pool(name="keep", bufs=1))
        small = ctx.enter_context(tc.tile_pool(name="small", bufs=8))
        work = ctx.enter_context(tc.tile_pool(name="work", bufs=2))
        grpool = ctx.enter_context(tc.tile_pool(name="grpool", bufs=1))
        ps_xt = ctx.enter_context(tc.psum_pool(name="ps_xt", bufs=4))
        ps = ctx.enter_context(tc.psum_pool(name="ps", bufs=1))

        pro = keep.tile([P, 512], BF16, name="pro")
        nc.scalar.dma_start(out=pro[:], in_=proto_emb.rearrange("n k c -> (n k) c"))
        xs = []
        for b in range(NB):
            xb = keep.tile([P, 4, 1024], BF16, name="x%d" % b)
            src = image_feat[b].rearrange("(p t) h w -> p t (h w)", t=4)
            if b == 0:
                for lo, hi in ((0, 256), (256, 512), (512, 1024)):
                    nc.sync.dma_start(out=xb[:, :, lo:hi], in_=src[:, :, lo:hi])
            else:
                nc.sync.dma_start(out=xb[:], in_=src)
            xs.append(xb)

        eps = keep.tile([P, 1], F32, name="eps")
        nc.vector.memset(eps[:], EPS)
        warm = keep.tile([P, 1], F32, name="warm")
        nc.scalar.activation(out=warm[:], in_=eps[:], func=ACT.Abs_reciprocal_sqrt)
        ident_f = keep.tile([P, P], F32, name="ident_f")
        make_identity(nc, ident_f[:])
        ident_b = keep.tile([P, P], BF16, name="ident_b")
        make_identity(nc, ident_b[:])

        res_max = keep.tile([P, 512], F32, name="res_max")
        res_sum = keep.tile([P, 512], F32, name="res_sum")
        res_max_v = res_max[:].rearrange("p (b n a) -> p b n a", n=4, a=8)
        res_sum_v = res_sum[:].rearrange("p (b n a) -> p b n a", n=4, a=8)
        half_mean = keep.tile([P, 512], F32, name="half_mean")
        half_max = keep.tile([P, 512], F32, name="half_max")
        sim_t = keep.tile([P, 2, 2, P], F32, name="sim_t")
        sim_sb = keep.tile([P, 2, P, 2], F32, name="sim_sb")
        mask_sb = keep.tile([P, 2, P, 2], F32, name="mask_sb")
        dst0 = out_0.rearrange("b n (a r) w -> (b n a) (r w)", a=4).rearrange("(q p) f -> p q f", p=P)
        dst1 = out_1.rearrange("b n (a r) w -> (b n a) (r w)", a=4).rearrange("(q p) f -> p q f", p=P)

        pcodes = keep.tile([P, 384], U32, name="pcodes", align_bytes=64)
        pscl = keep.tile([P, 384], U8, name="pscl", align_bytes=64)

        def prototypes():
            psq = keep.tile([P, 512], F32, name="psq")
            pss = keep.tile([P, 1], F32, name="pss")
            nc.vector.scalar_tensor_tensor(
                out=psq[:], in0=pro[:], scalar=1.0, in1=pro[:],
                op0=ALU.mult, op1=ALU.mult, accum_out=pss[:],
            )
            prin = keep.tile([P, 1], F32, name="prin")
            nc.scalar.activation(
                out=prin[:], in_=pss[:], func=ACT.Abs_reciprocal_sqrt, bias=eps[:, 0:1]
            )
            pn = keep.tile([P, 4, P], BF16, name="pn")
            nc.vector.tensor_scalar(
                out=pn[:], in0=pro[:].rearrange("m (p t) -> m t p", t=4),
                scalar1=prin[:, 0:1], scalar2=None, op0=ALU.mult,
            )
            pt_ps = ps.tile([P, 4, P], BF16, name="pt_ps", tag="o")
            for t in range(4):
                nc.tensor.transpose(pt_ps[:, t, :], pn[:, t, :], ident_b[:])
            pgrp = keep.tile([P, 384, 4], BF16, name="pgrp", align_bytes=64)
            nc.vector.tensor_copy(out=pgrp[:, 256:384, :], in_=pt_ps[:].rearrange("p t m -> p m t"))
            for d in range(2):
                nc.vector.tensor_copy(
                    out=pgrp[:, 0:256, :].rearrange("p (s d q) t -> p d s q t", d=2, q=32)[:, d],
                    in_=pt_ps[:].rearrange("p t (q s) -> p s q t", s=4),
                )
            for lo, hi in ((256, 384), (0, 256)):
                nc.vector.quantize_mx(
                    out=pcodes[:, lo:hi].bitcast(FP8X4), scales=pscl[:, lo:hi],
                    in_=pgrp[:, lo:hi, :].rearrange("p m t -> p (m t)"),
                )

        xts = {}
        sss = {}
        rins = {}
        rbs = {}
        rss = {}
        grps = {}
        cds = {}
        outs = {}
        sums = {}
        xns = {}
        bks = {}

        def gf(b):
            return GF_LAST if b == LAST else GF

        def t1(k):
            if k >= 4 * NB:
                return
            b, u = divmod(k, 4)
            xw = xs[b][:].bitcast(F32)
            xt = ps_xt.tile([P, 512], F32, name="xt")
            for t in range(4):
                nc.tensor.transpose(
                    xt[:, 128 * t:128 * (t + 1)], xw[:, t, 128 * u:128 * (u + 1)], ident_f[:]
                )
            xts[k] = xt

        def sumsq(k, e):
            b, u = divmod(k, 4)
            h, j = divmod(u, 2)
            if j == 0 and e == 0:
                sss[(b, h)] = small.tile([P, 4], F32, name="ss")
            v = xts[k][:].bitcast(BF16).rearrange("p (c e) -> p c e", e=2)
            junk = work.tile([P, 512], BF16, name="junk")
            nc.scalar.activation(
                out=junk[:], in_=v[:, :, e], func=ACT.Square,
                accum_out=sss[(b, h)][:, 2 * j + e:2 * j + e + 1],
            )

        def root(b, h):
            rins[(b, h)] = small.tile([P, 4], F32, name="rin")
            nc.scalar.activation(
                out=rins[(b, h)][:], in_=sss[(b, h)][:], func=ACT.Abs_reciprocal_sqrt, bias=eps[:, 0:1]
            )

        def bcast_t(b, h, skip=()):
            rp = ps.tile([P, 2, 256], F32, name="rp", tag="rp%d" % h)
            for j in range(2):
                for e in range(2):
                    c = 2 * j + e
                    if c in skip:
                        continue
                    nc.tensor.transpose(
                        rp[:, e, 128 * j:128 * (j + 1)],
                        rins[(b, h)][:, c:c + 1].to_broadcast([P, P]), ident_f[:],
                    )
            rbs[(b, h)] = rp

        def rcopy(b):
            lo = gf(b)
            rs = work.tile([P, SF - lo], F32, name="rs")
            nc.scalar.copy(out=rs[:], in_=rbs[(b, 0)][:].rearrange("p e m -> p (e m)")[:, lo:SF])
            rss[b] = rs

        def scale(engine, b, h, e, lo, hi, rin):
            c0 = 512 * h + 256 * e
            engine.tensor_tensor(
                out=grps[b][:, 4 * (c0 + lo):4 * (c0 + hi)].rearrange("p (c i t) -> p c t i", i=RUN, t=4),
                in0=xs[b][:, :, 512 * h + 2 * lo:512 * h + 2 * hi]
                .rearrange("p t (c i e) -> p e c t i", i=RUN, e=2)[:, e],
                in1=rin.rearrange("p (c i) -> p c i", i=RUN)
                .unsqueeze(2).to_broadcast([P, (hi - lo) // RUN, 4, RUN]),
                op=ALU.mult,
            )

        def scale_g(b):
            grps[b] = grpool.tile([P, 4096], BF16, name="grp", align_bytes=64)
            lo = gf(b)
            if lo < 256:
                scale(nc.gpsimd, b, 0, 0, lo, 256, rss[b][:, 0:256 - lo])
            scale(nc.gpsimd, b, 0, 1, 0, SF - 256, rss[b][:, 256 - lo:SF - lo])

        def scale_v(b, h, e, lo, hi):
            scale(nc.vector, b, h, e, lo, hi, rbs[(b, h)][:, e, lo:hi])

        def scale_s(b, h, j, e):
            xn = work.tile([P, 512], BF16, name="xn")
            v = xts[4 * b + 2 * h + j][:].bitcast(BF16).rearrange("m (u f p e) -> m e u p f", u=2, f=2, e=2)
            nc.scalar.activation(
                out=xn[:].rearrange("m (u p f) -> m u p f", u=2, f=2), in_=v[:, e],
                func=ACT.Copy, scale=rins[(b, h)][:, 2 * j + e:2 * j + e + 1],
            )
            xns[(b, h, j, e)] = xn

        def back_t(b, h, j, e):
            bk = ps_xt.tile([P, 2, P], F32, name="xt")
            words = xns[(b, h, j, e)][:].bitcast(F32)
            for u in range(2):
                nc.tensor.transpose(bk[:, u, :], words[:, 128 * u:128 * (u + 1)], ident_f[:])
            bks[(b, h, j, e)] = bk

        def back_copy(b, h, j, e):
            c0 = 512 * h + 256 * e + 128 * j
            out = grps[b][:, 4 * c0:4 * (c0 + 128)].bitcast(F32).rearrange("p (m u) -> p m u", u=2)
            in_ = bks[(b, h, j, e)][:].rearrange("p u m -> p m u")
            nc.scalar.copy(out=out, in_=in_)

        def quant(b, h0, h1):
            if h0 == 0:
                codes = work.tile([P, 1024], U32, name="codes", align_bytes=64)
                scl = work.tile([P, 1024], U8, name="scl", align_bytes=64)
                cds[b] = (codes, scl)
            codes, scl = cds[b]
            cols = slice(512 * h0, 512 * h1)
            nc.vector.quantize_mx(
                out=codes[:, cols].bitcast(FP8X4), scales=scl[:, cols],
                in_=grps[b][:, 2048 * h0:2048 * h1],
            )

        def mx(b, h, out, col, pcol, start, stop):
            codes, scl = cds[b]
            nc.tensor.matmul_mx(
                out=out[:, col:col + 128],
                lhsT=codes[:, h:h + 128].bitcast(FP8X4), lhsT_scale=scl[:, h:h + 128],
                rhs=pcodes[:, pcol:pcol + 128].bitcast(FP8X4), rhs_scale=pscl[:, pcol:pcol + 128],
                start=start, stop=stop,
            )

        def mx_all(b, h, tag):
            o = ps.tile([P, 512], F32, name="o", tag=tag)
            for j in range(4):
                mx(b, 512 * h + 128 * j, o, 128 * j, 256, True, True)
            outs[(b, h)] = o

        def mx_sum(b, h):
            if h == 0:
                sums[b] = ps.tile([P, 512], F32, name="sm")
            for j in range(4 * h, 4 * h + 4):
                for s in range(4):
                    mx(b, 128 * j, sums[b], 32 * j, 64 * s, s == 0, s == 3)

        def top(b, h):
            nc.vector.tensor_reduce(
                out=res_max_v[:, b, :, 4 * h:4 * h + 4].rearrange("p n j -> p j n"),
                in_=outs[(b, h)][:].rearrange("p (j n k) -> p j n k", n=4, k=32),
                axis=AX.X, op=ALU.max,
            )

        def add(b, j0=0):
            nc.vector.tensor_reduce(
                out=res_sum_v[:, b, :, j0:8].rearrange("p n j -> p j n"),
                in_=sums[b][:, 32 * j0:256].rearrange("p (j n g) -> p j n g", n=4, g=8),
                axis=AX.X, op=ALU.add,
            )

        def mix(engine, lo, hi):
            cols = slice(32 * lo, 32 * hi)
            q, x = divmod(lo, 8)
            for dst, src, factor in ((half_mean, res_sum, 1.0 / 64.0), (half_max, res_max, 0.5)):
                engine.tensor_scalar(
                    out=dst[:, cols], in0=src[:, cols],
                    scalar1=factor, scalar2=0.0, op0=ALU.mult, op1=ALU.add,
                )
            for e in range(2):
                engine.tensor_tensor(
                    out=sim_t[:, q, e, 16 * x:16 * (x + hi - lo)].rearrange("p (x j) -> p x j", j=2),
                    in0=half_max[:, cols].rearrange("p (x e j) -> p e x j", e=2, j=2)[:, e],
                    in1=half_mean[:, cols].rearrange("p (x e j) -> p e x j", e=2, j=2)[:, e],
                    op=ALU.add,
                )

        def fin_t(q):
            fin = ps_xt.tile([P, 2, P], F32, name="xt")
            for e in range(2):
                nc.tensor.transpose(fin[:, e, :], sim_t[:, q, e, :], ident_f[:])
            return fin[:].rearrange("p e m -> p m e")

        def ok(b):
            return 0 <= b < NB

        with tc.manual_schedule():
            t1(0)
            t1(1)
            prototypes()
            for r in range(NB):
                k = 4 * r
                t1(k + 2)
                if ok(r):
                    sumsq(k, 0)
                if ok(r - 1):
                    root(r - 1, 1)
                    bcast_t(r - 1, 1)
                    if r - 1 not in S_SKIP:
                        back_copy(r - 1, 0, 1, 1)
                t1(k + 3)
                if ok(r):
                    sumsq(k, 1)
                if ok(r - 2):
                    mx_all(r - 2, 0, "o")
                    mx_sum(r - 2, 0)
                if ok(r - 1):
                    scale_v(r - 1, 1, 0, 0, 256)
                if ok(r - 2):
                    top(r - 2, 0)
                if ok(r - 1):
                    scale_v(r - 1, 1, 1, 0, 256)
                    quant(r - 1, 0, 1)
                    quant(r - 1, 1, 2)
                if ok(r):
                    for e in range(2):
                        sumsq(k + 1, e)
                    sumsq(k + 2, 0)
                    root(r, 0)
                    bcast_t(r, 0, () if r in S_SKIP else (3,))
                if ok(r - 2):
                    mx_all(r - 2, 1, "o")
                    top(r - 2, 1)
                if ok(r):
                    sumsq(k + 2, 1)
                    if r not in S_SKIP:
                        scale_s(r, 0, 1, 1)
                        back_t(r, 0, 1, 1)
                t1(k + 4)
                t1(k + 5)
                if ok(r - 2):
                    mx_sum(r - 2, 1)
                if ok(r):
                    sumsq(k + 3, 0)
                    rcopy(r)
                    scale_g(r)
                    scale_v(r, 0, 0, 0, gf(r))
                    if r in S_SKIP:
                        scale_v(r, 0, 1, SF - 256, 256)
                    sumsq(k + 3, 1)
                if ok(r - 2):
                    add(r - 2)
                    if r - 2 == 7:
                        mix(nc.gpsimd, 0, 8)
                    if r - 2 == 13:
                        mix(nc.gpsimd, 8, 14)

            root(LAST, 1)
            bcast_t(LAST, 1, (1, 3))
            back_copy(LAST, 0, 1, 1)
            mx_all(LAST - 1, 0, "o")
            scale_v(LAST, 1, 0, 0, 256)
            for j in range(2):
                scale_s(LAST, 1, j, 1)
                back_t(LAST, 1, j, 1)
            mx_sum(LAST - 1, 0)
            top(LAST - 1, 0)
            for j in range(2):
                back_copy(LAST, 1, j, 1)
            mx_all(LAST - 1, 1, "o")
            mx_sum(LAST - 1, 1)
            quant(LAST, 0, 1)
            top(LAST - 1, 1)
            quant(LAST, 1, 2)
            fin = fin_t(0)
            nc.scalar.activation(out=mask_sb[:, 0], in_=fin, func=ACT.Sigmoid)
            nc.scalar.copy(out=sim_sb[:, 0], in_=fin)
            nc.sync.dma_start(out=dst0[:, 0, :], in_=mask_sb[:, 0].rearrange("p m e -> p (m e)"))
            nc.sync.dma_start(out=dst1[:, 0, :], in_=sim_sb[:, 0].rearrange("p m e -> p (m e)"))
            add(LAST - 1)
            mx_all(LAST, 0, "rp0")
            mx_all(LAST, 1, "rp1")
            sums[LAST] = ps.tile([P, 512], F32, name="sm")
            mx_sum(LAST, 1)
            top(LAST, 0)
            nc.vector.tensor_reduce(
                out=res_sum_v[:, LAST, :, 0:4].rearrange("p n j -> p j n"),
                in_=outs[(LAST, 0)][:].rearrange("p (j n k) -> p j n k", n=4, k=32),
                axis=AX.X, op=ALU.add,
            )
            top(LAST, 1)
            add(LAST, 4)
            mix(nc.vector, 14, NB)
            fin = fin_t(1)
            nc.scalar.activation(out=mask_sb[:, 1], in_=fin, func=ACT.Sigmoid)
            nc.vector.tensor_copy(out=sim_sb[:, 1], in_=fin)
            nc.sync.dma_start(out=dst0[:, 1, :], in_=mask_sb[:, 1].rearrange("p m e -> p (m e)"))
            nc.scalar.dma_start(out=dst1[:, 1, :], in_=sim_sb[:, 1].rearrange("p m e -> p (m e)"))
